import numpy as np
import ml_dtypes


def mxq(x, axis, fmt="e4m3"):
    dtype, down = {"e4m3": (ml_dtypes.float8_e4m3fn, 7), "e5m2": (ml_dtypes.float8_e5m2, 14)}[fmt]
    v = np.moveaxis(np.asarray(x, np.float32).astype(ml_dtypes.bfloat16).astype(np.float64), axis, -1)
    blocks = v.reshape(v.shape[:-1] + (-1, 32))
    amax = np.abs(blocks).max(-1, keepdims=True)
    byte = np.maximum(np.where(amax > 0, np.frexp(amax)[1] - 1 + 127, 0) - down, 1)
    scale = np.exp2(byte - 127.0)
    codes = (blocks / scale).astype(np.float32).astype(dtype).astype(np.float64)
    return np.moveaxis((codes * scale).reshape(v.shape), -1, axis)


WIDE = False


def mx_kscale(k):
    if not WIDE:
        return np.ones(k)
    levels = np.array([10, -10, 5, -5, 0])
    if k % 512:
        return np.exp2(np.random.permutation(np.resize(levels, k // 32))).repeat(32)
    a = np.empty((k // 512, 16))
    for p in range(k // 512):
        a[p, :8] = np.random.permutation(np.resize(levels, 8))
        for g in range(8):
            far = levels[np.abs(levels - a[p, g]) >= 10]
            a[p, g + 8] = far[np.random.randint(len(far))]
    return np.exp2(a.ravel()).repeat(32)


BF16 = ml_dtypes.bfloat16


def bf(x):
    return np.asarray(x, np.float32).astype(BF16)


def f64(x):
    return np.asarray(x).astype(np.float64)


B, DIN, DOUT = 1024, 2048, 2048

MIN_NORM = 1e-15
PROJ_EPS = 1e-3
W_MUL = 0.1
B_MUL = 0.1
C = 1.0


def artanh(x):
    x = np.clip(x, -1.0 + 1e-5, 1.0 - 1e-5)
    return 0.5 * (np.log1p(x) - np.log1p(-x))


def mobius_matvec(w, x, c):
    sqrt_c = c ** 0.5
    x_norm = np.maximum(np.linalg.norm(x, axis=-1, keepdims=True), MIN_NORM)
    mx = mxq(x, 1, "e4m3") @ mxq(w, 1, "e4m3").T
    mx_norm = np.maximum(np.linalg.norm(mx, axis=-1, keepdims=True), MIN_NORM)
    res = np.tanh(mx_norm / x_norm * artanh(sqrt_c * x_norm)) * mx / (mx_norm * sqrt_c)
    zero_row = np.all(mx == 0, axis=-1, keepdims=True)
    return np.where(zero_row, 0.0, res)


def expmap0(u, c):
    sqrt_c = c ** 0.5
    u_norm = np.maximum(np.linalg.norm(u, axis=-1, keepdims=True), MIN_NORM)
    return np.tanh(sqrt_c * u_norm) * u / (sqrt_c * u_norm)


def mobius_add(x, y, c):
    x2 = np.sum(x * x, axis=-1, keepdims=True)
    y2 = np.sum(y * y, axis=-1, keepdims=True)
    xy = np.sum(x * y, axis=-1, keepdims=True)
    num = (1 + 2 * c * xy + c * y2) * x + (1 - c * x2) * y
    denom = 1 + 2 * c * xy + c * c * x2 * y2
    return num / np.maximum(denom, MIN_NORM)


def project(x, c):
    sqrt_c = c ** 0.5
    norm = np.maximum(np.linalg.norm(x, axis=-1, keepdims=True), MIN_NORM)
    maxnorm = (1.0 - PROJ_EPS) / sqrt_c
    return np.where(norm > maxnorm, x / norm * maxnorm, x)


def setup_inputs():
    s = mx_kscale(DIN)
    g = np.exp2(np.ceil(np.log2(np.sqrt(np.mean(s * s)))))
    return {"x": bf(np.random.standard_normal((B, DIN)) * 0.7 / np.sqrt(DIN) * s / g),
            "weight": bf(np.random.standard_normal((DOUT, DIN)) * 10.0 / np.sqrt(DOUT) * g / s),
            "bias": bf(np.random.standard_normal(DOUT) * 3.0 / np.sqrt(DOUT))}


def reference(x, weight, bias):
    c = C
    w_lr = f64(weight) * W_MUL
    mv = mobius_matvec(w_lr, f64(x), c)
    b = expmap0(f64(bias) * B_MUL, c)
    out = project(mobius_add(mv, b[None, :], 1.0), c)
    return np.where(out >= 0, out, 0.2 * out)

@@ -1,0 +1,309 @@
+from contextlib import ExitStack
+
+import concourse.bass as bass
+import concourse.mybir as mybir
+import concourse.tile as tile
+from concourse.masks import make_identity
+
+F32 = mybir.dt.float32
+BF16 = mybir.dt.bfloat16
+U32 = mybir.dt.uint32
+U8 = mybir.dt.uint8
+FP8X4 = mybir.dt.float8_e4m3fn_x4
+ALU = mybir.AluOpType
+ACT = mybir.ActivationFunctionType
+AX = mybir.AxisListType
+
+P = 128
+B, DIN, DOUT = 1024, 2048, 2048
+FLOPS = 2 * B * DIN * DOUT
+NG = DIN // 512
+NT = B // P
+NB = DOUT // 512
+PINNED = False
+
+
+def tile_hypequalizedlinear_kernel(tc, x, weight, bias, out):
+    nc = tc.nc
+    x_v = x.rearrange("(c a p) k -> c p a k", a=2, p=P)
+    w_v = weight.rearrange("(c a p) k -> c p a k", a=2, p=P)
+    out_v = out.rearrange("(t p) n -> t p n", p=P)
+
+    with ExitStack() as ctx:
+        if PINNED:
+            ctx.enter_context(tc.manual_schedule())
+        const = ctx.enter_context(tc.tile_pool(name="const", bufs=1))
+        xin = ctx.enter_context(tc.tile_pool(name="xin", bufs=4))
+        win = ctx.enter_context(tc.tile_pool(name="win", bufs=4))
+        gxp = ctx.enter_context(tc.tile_pool(name="gxp", bufs=2))
+        gwp = ctx.enter_context(tc.tile_pool(name="gwp", bufs=3))
+        tpl = ctx.enter_context(tc.tile_pool(name="tpl", bufs=3))
+        jkp = ctx.enter_context(tc.tile_pool(name="jkp", bufs=4))
+        sm = ctx.enter_context(tc.tile_pool(name="sm", bufs=3))
+        psum = ctx.enter_context(tc.psum_pool(name="psum", bufs=1))
+
+        ident = const.tile([P, P], F32, name="ident")
+        make_identity(nc, ident[:])
+        mh8 = const.tile([P, 8], F32, name="mh8")
+        nc.gpsimd.memset(mh8[:], -0.5)
+        ex2 = const.tile([P, 2], F32, name="ex2")
+        nc.gpsimd.memset(ex2[:, 0:1], -1.0)
+        nc.gpsimd.memset(ex2[:, 1:2], -0.5)
+
+        bias_bc = const.tile([P, DOUT], BF16, name="bias_bc")
+        b_bc = const.tile([P, DOUT], F32, name="b_bc")
+        xc = const.tile([P, 4, NG, 256], U32, name="xc", align_bytes=64)
+        xs = const.tile([P, 4, NG, 256], U8, name="xs", align_bytes=64)
+        wc = const.tile([P, NG, DOUT], U32, name="wc", align_bytes=64)
+        ws = const.tile([P, NG, DOUT], U8, name="ws", align_bytes=64)
+        xn2 = const.tile([P, NT], F32, name="xn2")
+        q = const.tile([P, NT], F32, name="q")
+        y2 = const.tile([P, 1], F32, name="y2")
+        c2 = const.tile([P, 1], F32, name="c2")
+
+        state = {"bank": 0}
+
+        def transposes(src, g):
+            bk = 4 + state["bank"] % 4
+            state["bank"] += 1
+            tp = psum.tile([P, 2, 2, P], F32, tag="bk%d" % bk, name="tp")
+            words = src[:].bitcast(F32)
+            for u in range(2):
+                for a in range(2):
+                    lo = 256 * g
+                    nc.tensor.transpose(tp[:, u, a, :], words[:, a, lo + u:lo + 256:2], ident[:])
+            return tp
+
+        def x_pair(c, src):
+            gx = gxp.tile([P, NG, 256, 4], BF16, name="gx", align_bytes=64)
+            gxw = gx[:].bitcast(F32)
+            for g in range(NG):
+                tp = transposes(src, g)
+                nc.scalar.copy(out=gxw[:, g, :, :], in_=tp[:].rearrange("p u a r -> p (a r) u"))
+            nc.vector.quantize_mx(
+                out=xc[:, c, :, :].rearrange("p g j -> p (g j)").bitcast(FP8X4),
+                scales=xs[:, c, :, :].rearrange("p g j -> p (g j)"),
+                in_=gx[:].rearrange("p g j t -> p (g j t)"),
+            )
+            for a in range(2):
+                jx = jkp.tile([P, DIN], BF16, name="jx", tag="jx", bufs=2)
+                nc.scalar.activation(out=jx[:], in_=src[:, a, :], func=ACT.Square,
+                                     accum_out=xn2[:, 2 * c + a:2 * c + a + 1])
+
+        def w_pair(c, src):
+            gw = gwp.tile([P, NG, 256, 4], BF16, name="gw", align_bytes=64)
+            for g in range(NG):
+                tp = transposes(src, g)
+                nc.vector.tensor_scalar(
+                    out=gw[:, g, :, :].rearrange("p j (u e) -> p j u e", e=2),
+                    in0=tp[:].bitcast(BF16).rearrange("p u a (r e) -> p (a r) u e", e=2),
+                    scalar1=0.1, scalar2=None, op0=ALU.mult,
+                )
+            for g in range(NG):
+                nc.vector.quantize_mx(
+                    out=wc[:, g, 256 * c:256 * c + 256].bitcast(FP8X4),
+                    scales=ws[:, g, 256 * c:256 * c + 256],
+                    in_=gw[:, g, :, :].rearrange("p j t -> p (j t)"),
+                )
+
+        banks = {}
+
+        def mx_block(r, n):
+            acc = psum.tile([P, 512], F32, tag="bk%d" % (4 * (r % 2) + n), name="acc")
+            banks[(r, n)] = acc
+            c, a = r // 2, r % 2
+            for g in range(NG):
+                nc.tensor.matmul_mx(
+                    out=acc[:],
+                    lhsT=xc[:, c, g, 128 * a:128 * a + 128].bitcast(FP8X4),
+                    lhsT_scale=xs[:, c, g, 128 * a:128 * a + 128],
+                    rhs=wc[:, g, 512 * n:512 * n + 512].bitcast(FP8X4),
+                    rhs_scale=ws[:, g, 512 * n:512 * n + 512],
+                    start=(g == 0), stop=(g == NG - 1),
+                )
+
+        def load(pool, view, c, nm):
+            t = pool.tile([P, 2, DIN], BF16, name=nm, tag=nm)
+            nc.sync.dma_start(out=t[:], in_=view[c])
+            return t
+
+        order = [("x", 0), ("w", 0), ("w", 1), ("b", 0), ("x", 1), ("w", 2), ("w", 3),
+                 ("x", 2), ("w", 4), ("w", 5), ("x", 3), ("w", 6), ("w", 7)]
+        loaded = {}
+        for kind, c in order:
+            if kind == "x":
+                loaded[(kind, c)] = load(xin, x_v, c, "xt")
+            elif kind == "w":
+                loaded[(kind, c)] = load(win, w_v, c, "wt")
+            else:
+                nc.sync.dma_start(out=bias_bc[:], in_=bias.partition_broadcast(P))
+
+        def xn_batch():
+            xc2 = sm.tile([P, NT], F32, name="xc2", bufs=1)
+            nc.gpsimd.tensor_scalar(out=xc2[:], in0=xn2[:], scalar1=1e-30, scalar2=None, op0=ALU.max)
+            rxn = sm.tile([P, NT], F32, name="rxn", bufs=1)
+            nc.gpsimd.tensor_tensor(out=rxn[:], in0=xc2[:], in1=mh8[:], op=ALU.pow)
+            v = sm.tile([P, NT], F32, name="v", bufs=1)
+            nc.vector.tensor_tensor(out=v[:], in0=xc2[:], in1=rxn[:], op=ALU.mult)
+            nc.vector.tensor_scalar(out=v[:], in0=v[:], scalar1=1.0 - 1e-5, scalar2=None, op0=ALU.min)
+            l1 = sm.tile([P, NT], F32, name="l1", bufs=1)
+            l2 = sm.tile([P, NT], F32, name="l2", bufs=1)
+            nc.scalar.activation(out=l1[:], in_=v[:], func=ACT.Ln, bias=1.0, scale=1.0)
+            nc.scalar.activation(out=l2[:], in_=v[:], func=ACT.Ln, bias=1.0, scale=-1.0)
+            nc.vector.tensor_tensor(out=l1[:], in0=l1[:], in1=l2[:], op=ALU.subtract)
+            nc.vector.scalar_tensor_tensor(out=q[:], in0=l1[:], scalar=0.5, in1=rxn[:],
+                                           op0=ALU.mult, op1=ALU.mult)
+
+        def bias_map():
+            sb = sm.tile([P, 1], F32, name="sb", bufs=1)
+            nc.scalar.activation(out=b_bc[:], in_=bias_bc[:], func=ACT.Square, accum_out=sb[:])
+            u2 = sm.tile([P, 1], F32, name="u2", bufs=1)
+            nc.gpsimd.tensor_scalar(out=u2[:], in0=sb[:], scalar1=0.01, scalar2=1e-30,
+                                    op0=ALU.mult, op1=ALU.max)
+            run = sm.tile([P, 1], F32, name="run", bufs=1)
+            nc.gpsimd.tensor_tensor(out=run[:], in0=u2[:], in1=mh8[:, 0:1], op=ALU.pow)
+            tb = sm.tile([P, 1], F32, name="tb", bufs=1)
+            nc.scalar.activation(out=tb[:], in_=u2[:], func=ACT.Tanh, scale=run[:, 0:1])
+            scb = sm.tile([P, 1], F32, name="scb", bufs=1)
+            nc.vector.tensor_scalar(out=scb[:], in0=tb[:], scalar1=run[:, 0:1], scalar2=0.1,
+                                    op0=ALU.mult, op1=ALU.mult)
+            nc.vector.tensor_tensor(out=y2[:], in0=tb[:], in1=tb[:], op=ALU.mult)
+            nc.vector.tensor_scalar(out=c2[:], in0=y2[:], scalar1=-1.0, scalar2=None, op0=ALU.add)
+            nc.vector.tensor_scalar(out=b_bc[:], in0=bias_bc[:], scalar1=scb[:, 0:1], scalar2=None,
+                                    op0=ALU.mult)
+
+        for kind, c in order:
+            if kind == "x":
+                x_pair(c, loaded[(kind, c)])
+                if c == 3:
+                    xn_batch()
+                    bias_map()
+            elif kind == "w":
+                w_pair(c, loaded[(kind, c)])
+                if c % 2 == 1:
+                    mx_block(0, c // 2)
+
+        sums = {}
+        coef = {}
+        tts = {}
+
+        def sums_of(r):
+            ssq = sm.tile([P, NB], F32, name="ssq")
+            dot = sm.tile([P, NB], F32, name="dot")
+            sums[r] = (ssq, dot)
+            for n in range(NB):
+                acc = banks[(r, n)]
+                jk = jkp.tile([P, 512], F32, name="jk", tag="jk")
+                nc.scalar.activation(out=jk[:], in_=acc[:], func=ACT.Square,
+                                     accum_out=ssq[:, n:n + 1])
+                nc.vector.scalar_tensor_tensor(out=jk[:], in0=acc[:], scalar=2.0,
+                                               in1=b_bc[:, 512 * n:512 * n + 512],
+                                               op0=ALU.mult, op1=ALU.mult,
+                                               accum_out=dot[:, n:n + 1])
+
+        def col(nm):
+            return sm.tile([P, 1], F32, name=nm, tag=nm)
+
+        def chain_stages(r):
+            ssq, dot = sums[r]
+            ce = nc.vector
+            loc = {}
+
+            def st_a():
+                y = col("y")
+                nc.vector.tensor_reduce(out=y[:], in_=ssq[:], axis=AX.X, op=ALU.add)
+                d2 = col("d2")
+                nc.vector.tensor_reduce(out=d2[:], in_=dot[:], axis=AX.X, op=ALU.add)
+                yc = col("yc")
+                nc.gpsimd.tensor_scalar(out=yc[:], in0=y[:], scalar1=1e-30, scalar2=None, op0=ALU.max)
+                rmn = col("rmn")
+                nc.gpsimd.tensor_tensor(out=rmn[:], in0=yc[:], in1=mh8[:, 0:1], op=ALU.pow)
+                sq = col("sq")
+                nc.gpsimd.tensor_scalar(out=sq[:], in0=rmn[:], scalar1=q[:, r:r + 1], scalar2=None,
+                                        op0=ALU.mult)
+                th = col("th")
+                nc.scalar.activation(out=th[:], in_=yc[:], func=ACT.Tanh, scale=sq[:, 0:1])
+                loc["d2"], loc["rmn"], loc["th"] = d2, rmn, th
+
+            def st_b():
+                th, rmn, d2 = loc["th"], loc["rmn"], loc["d2"]
+                s = col("s")
+                ce.tensor_scalar(out=s[:], in0=th[:], scalar1=rmn[:, 0:1], scalar2=None, op0=ALU.mult)
+                x2 = col("x2")
+                ce.tensor_scalar(out=x2[:], in0=th[:], scalar1=th[:, 0:1], scalar2=None, op0=ALU.mult)
+                e1 = col("e1")
+                ce.tensor_scalar(out=e1[:], in0=s[:], scalar1=d2[:, 0:1], scalar2=1.0,
+                                 op0=ALU.mult, op1=ALU.add)
+                pk = sm.tile([P, 2], F32, name="pk", tag="pk")
+                den = col("den")
+                ce.tensor_scalar(out=den[:], in0=x2[:], scalar1=y2[:, 0:1], scalar2=e1[:, 0:1],
+                                 op0=ALU.mult, op1=ALU.add)
+                num = col("num")
+                ce.tensor_scalar(out=num[:], in0=x2[:], scalar1=c2[:, 0:1], scalar2=e1[:, 0:1],
+                                 op0=ALU.add, op1=ALU.add)
+                ce.tensor_scalar(out=pk[:, 0:1], in0=den[:], scalar1=1e-15, scalar2=None, op0=ALU.max)
+                ce.tensor_scalar(out=pk[:, 1:2], in0=num[:], scalar1=pk[:, 0:1], scalar2=1e-30,
+                                 op0=ALU.mult, op1=ALU.max)
+                pw = sm.tile([P, 2], F32, name="pw", tag="pw")
+                nc.gpsimd.tensor_tensor(out=pw[:], in0=pk[:], in1=ex2[:], op=ALU.pow)
+                asx = col("asx")
+                ce.tensor_scalar(out=asx[:], in0=e1[:], scalar1=y2[:, 0:1], scalar2=s[:, 0:1],
+                                 op0=ALU.add, op1=ALU.mult)
+                bc = col("bc")
+                ce.tensor_scalar(out=bc[:], in0=x2[:], scalar1=-1.0, scalar2=1.0,
+                                 op0=ALU.mult, op1=ALU.add)
+                loc["pw"], loc["asx"], loc["bc"] = pw, asx, bc
+
+            def st_c():
+                pw, asx, bc = loc["pw"], loc["asx"], loc["bc"]
+                pr = col("pr")
+                ce.tensor_scalar(out=pr[:], in0=pw[:, 1:2], scalar1=0.999, scalar2=pw[:, 0:1],
+                                 op0=ALU.mult, op1=ALU.min)
+                al = col("al")
+                ce.tensor_scalar(out=al[:], in0=asx[:], scalar1=pr[:, 0:1], scalar2=None, op0=ALU.mult)
+                be = col("be")
+                ce.tensor_scalar(out=be[:], in0=bc[:], scalar1=pr[:, 0:1], scalar2=None, op0=ALU.mult)
+                coef[r] = (al, be)
+
+            return [st_a, st_b, st_c]
+
+        def scale_rows(r):
+            al, be = coef[r]
+            t = tpl.tile([P, DOUT], F32, name="t", tag="t")
+            tts[r] = t
+            for n in range(NB):
+                nc.scalar.activation(out=t[:, 512 * n:512 * n + 512], in_=banks[(r, n)][:],
+                                     func=ACT.Copy, scale=al[:, 0:1])
+
+        def add_bias(r, h):
+            al, be = coef[r]
+            t = tts[r]
+            sl = slice(1024 * h, 1024 * h + 1024)
+            nc.vector.scalar_tensor_tensor(out=t[:, sl], in0=b_bc[:, sl], scalar=be[:, 0:1],
+                                           in1=t[:, sl], op0=ALU.mult, op1=ALU.add)
+
+        def leaky_store(r, h):
+            t = tts[r]
+            sl = slice(1024 * h, 1024 * h + 1024)
+            nc.vector.scalar_tensor_tensor(out=t[:, sl], in0=t[:, sl], scalar=0.2,
+                                           in1=t[:, sl], op0=ALU.mult, op1=ALU.max)
+            nc.sync.dma_start(out=out_v[r][:, sl], in_=t[:, sl])
+
+        for r in range(NT + 1):
+            if r < NT:
+                if r > 0:
+                    for n in range(NB):
+                        mx_block(r, n)
+                sums_of(r)
+            stages = chain_stages(r) if r < NT else []
+            if r > 0:
+                scale_rows(r - 1)
+            big = []
+            if r > 0:
+                big = [lambda: add_bias(r - 1, 0), lambda: add_bias(r - 1, 1),
+                       lambda: leaky_store(r - 1, 0), lambda: leaky_store(r - 1, 1)]
+            for i in range(4):
+                if i < len(stages):
+                    stages[i]()
+                if i < len(big):
+                    big[i]()

@@ -12,7 +12,6 @@ U8 = mybir.dt.uint8
 FP8X4 = mybir.dt.float8_e4m3fn_x4
 ALU = mybir.AluOpType
 ACT = mybir.ActivationFunctionType
-AX = mybir.AxisListType
 
 P = 128
 B, DIN, DOUT = 1024, 2048, 2048
@@ -20,7 +19,11 @@ FLOPS = 2 * B * DIN * DOUT
 NG = DIN // 512
 NT = B // P
 NB = DOUT // 512
-PINNED = False
+
+ORDER = [("x", 0), ("w", 0), ("w", 1), ("x", 1), ("w", 2), ("x", 2), ("w", 3), ("x", 3),
+         ("w", 4), ("w", 5), ("w", 6), ("w", 7)]
+V_GROUPS = [3, 3, 3, 3, 3, 2, 2, 2]
+AHEAD = 5
 
 
 def tile_hypequalizedlinear_kernel(tc, x, weight, bias, out):
@@ -30,81 +33,103 @@ def tile_hypequalizedlinear_kernel(tc, x, weight, bias, out):
     out_v = out.rearrange("(t p) n -> t p n", p=P)
 
     with ExitStack() as ctx:
-        if PINNED:
-            ctx.enter_context(tc.manual_schedule())
         const = ctx.enter_context(tc.tile_pool(name="const", bufs=1))
         xin = ctx.enter_context(tc.tile_pool(name="xin", bufs=4))
-        win = ctx.enter_context(tc.tile_pool(name="win", bufs=4))
-        gxp = ctx.enter_context(tc.tile_pool(name="gxp", bufs=2))
-        gwp = ctx.enter_context(tc.tile_pool(name="gwp", bufs=3))
-        tpl = ctx.enter_context(tc.tile_pool(name="tpl", bufs=3))
-        jkp = ctx.enter_context(tc.tile_pool(name="jkp", bufs=4))
-        sm = ctx.enter_context(tc.tile_pool(name="sm", bufs=3))
+        win = ctx.enter_context(tc.tile_pool(name="win", bufs=5))
+        gp = ctx.enter_context(tc.tile_pool(name="gp", bufs=3))
+        zp = ctx.enter_context(tc.tile_pool(name="zp", bufs=3))
+        jkp = ctx.enter_context(tc.tile_pool(name="jkp", bufs=2))
+        sm = ctx.enter_context(tc.tile_pool(name="sm", bufs=4))
         psum = ctx.enter_context(tc.psum_pool(name="psum", bufs=1))
+        ctx.enter_context(tc.manual_schedule())
 
         ident = const.tile([P, P], F32, name="ident")
         make_identity(nc, ident[:])
-        mh8 = const.tile([P, 8], F32, name="mh8")
+        mh8 = const.tile([P, NT], F32, name="mh8")
         nc.gpsimd.memset(mh8[:], -0.5)
-        ex2 = const.tile([P, 2], F32, name="ex2")
-        nc.gpsimd.memset(ex2[:, 0:1], -1.0)
-        nc.gpsimd.memset(ex2[:, 1:2], -0.5)
+        m1 = const.tile([P, 1], F32, name="m1")
+        nc.gpsimd.memset(m1[:], -1.0)
+        ones = const.tile([P, P], F32, name="ones")
+        nc.gpsimd.memset(ones[:], 1.0)
 
         bias_bc = const.tile([P, DOUT], BF16, name="bias_bc")
-        b_bc = const.tile([P, DOUT], F32, name="b_bc")
+        bias_p = const.tile([P, DOUT // P], BF16, name="bias_p")
         xc = const.tile([P, 4, NG, 256], U32, name="xc", align_bytes=64)
         xs = const.tile([P, 4, NG, 256], U8, name="xs", align_bytes=64)
         wc = const.tile([P, NG, DOUT], U32, name="wc", align_bytes=64)
         ws = const.tile([P, NG, DOUT], U8, name="ws", align_bytes=64)
-        xn2 = const.tile([P, NT], F32, name="xn2")
+        xn2 = const.tile([P, 2, NT], F32, name="xn2")
         q = const.tile([P, NT], F32, name="q")
         y2 = const.tile([P, 1], F32, name="y2")
-        c2 = const.tile([P, 1], F32, name="c2")
+        y21 = const.tile([P, 1], F32, name="y21")
+        scb = const.tile([P, 1], F32, name="scb")
+        scb2 = const.tile([P, 1], F32, name="scb2")
 
-        state = {"bank": 0}
+        raw = {}
 
-        def transposes(src, g):
-            bk = 4 + state["bank"] % 4
-            state["bank"] += 1
-            tp = psum.tile([P, 2, 2, P], F32, tag="bk%d" % bk, name="tp")
-            words = src[:].bitcast(F32)
-            for u in range(2):
-                for a in range(2):
-                    lo = 256 * g
-                    nc.tensor.transpose(tp[:, u, a, :], words[:, a, lo + u:lo + 256:2], ident[:])
-            return tp
+        def load(i):
+            kind, c = ORDER[i]
+            view = x_v if kind == "x" else w_v
+            pool = xin if kind == "x" else win
+            t = pool.tile([P, 2, DIN], BF16, name="raw_" + kind, tag="raw_" + kind)
+            raw[i] = t
+            if i < 2:
+                for h in range(2):
+                    sl = slice(1024 * h, 1024 * h + 1024)
+                    nc.sync.dma_start(out=t[:, :, sl], in_=view[c][:, :, sl])
+            else:
+                nc.sync.dma_start(out=t[:], in_=view[c])
 
-        def x_pair(c, src):
-            gx = gxp.tile([P, NG, 256, 4], BF16, name="gx", align_bytes=64)
-            gxw = gx[:].bitcast(F32)
+        grouped = {}
+
+        def premult(i):
+            kind, c = ORDER[i]
+            if kind == "w":
+                lo = 512 * V_GROUPS[c]
+                if lo < DIN:
+                    nc.vector.tensor_scalar(out=raw[i][:, :, lo:], in0=raw[i][:, :, lo:], scalar1=0.1,
+                                            scalar2=None, op0=ALU.mult)
+
+        def transpose_and_copy(i):
+            kind, c = ORDER[i]
+            words = raw[i][:].bitcast(F32)
+            gt = gp.tile([P, NG, 256, 4], BF16, name="gt", align_bytes=64)
+            grouped[i] = gt
             for g in range(NG):
-                tp = transposes(src, g)
-                nc.scalar.copy(out=gxw[:, g, :, :], in_=tp[:].rearrange("p u a r -> p (a r) u"))
-            nc.vector.quantize_mx(
-                out=xc[:, c, :, :].rearrange("p g j -> p (g j)").bitcast(FP8X4),
-                scales=xs[:, c, :, :].rearrange("p g j -> p (g j)"),
-                in_=gx[:].rearrange("p g j t -> p (g j t)"),
-            )
-            for a in range(2):
-                jx = jkp.tile([P, DIN], BF16, name="jx", tag="jx", bufs=2)
-                nc.scalar.activation(out=jx[:], in_=src[:, a, :], func=ACT.Square,
-                                     accum_out=xn2[:, 2 * c + a:2 * c + a + 1])
+                tp = psum.tile([P, 2, 2, P], F32, tag="bk%d" % (4 + g), name="tp")
+                for u in range(2):
+                    for a in range(2):
+                        nc.tensor.transpose(tp[:, u, a, :], words[:, a, 256 * g + u:256 * g + 256:2],
+                                            ident[:])
+                if kind == "w" and g < V_GROUPS[c]:
+                    nc.vector.tensor_scalar(
+                        out=gt[:, g, :, :].rearrange("p j (u e) -> p j u e", e=2),
+                        in0=tp[:].bitcast(BF16).rearrange("p u a (r e) -> p (a r) u e", e=2),
+                        scalar1=0.1, scalar2=None, op0=ALU.mult)
+                else:
+                    nc.scalar.copy(out=gt[:, g, :, :].bitcast(F32),
+                                   in_=tp[:].rearrange("p u a r -> p (a r) u"))
 
-        def w_pair(c, src):
-            gw = gwp.tile([P, NG, 256, 4], BF16, name="gw", align_bytes=64)
-            for g in range(NG):
-                tp = transposes(src, g)
-                nc.vector.tensor_scalar(
-                    out=gw[:, g, :, :].rearrange("p j (u e) -> p j u e", e=2),
-                    in0=tp[:].bitcast(BF16).rearrange("p u a (r e) -> p (a r) u e", e=2),
-                    scalar1=0.1, scalar2=None, op0=ALU.mult,
-                )
-            for g in range(NG):
+        def quantise(i):
+            kind, c = ORDER[i]
+            gt = grouped[i]
+            if kind == "x":
                 nc.vector.quantize_mx(
-                    out=wc[:, g, 256 * c:256 * c + 256].bitcast(FP8X4),
-                    scales=ws[:, g, 256 * c:256 * c + 256],
-                    in_=gw[:, g, :, :].rearrange("p j t -> p (j t)"),
-                )
+                    out=xc[:, c, :, :].rearrange("p g j -> p (g j)").bitcast(FP8X4),
+                    scales=xs[:, c, :, :].rearrange("p g j -> p (g j)"),
+                    in_=gt[:].rearrange("p g j t -> p (g j t)"))
+            else:
+                for g in range(NG):
+                    nc.vector.quantize_mx(
+                        out=wc[:, g, 256 * c:256 * c + 256].bitcast(FP8X4),
+                        scales=ws[:, g, 256 * c:256 * c + 256],
+                        in_=gt[:, g, :, :].rearrange("p j t -> p (j t)"))
+
+        def x_norm(i, a, h):
+            c = ORDER[i][1]
+            jx = jkp.tile([P, 1024], BF16, name="jx", tag="jx")
+            nc.scalar.activation(out=jx[:], in_=raw[i][:, a, 1024 * h:1024 * h + 1024], func=ACT.Square,
+                                 accum_out=xn2[:, h, 2 * c + a:2 * c + a + 1])
 
         banks = {}
 
@@ -119,191 +144,240 @@ def tile_hypequalizedlinear_kernel(tc, x, weight, bias, out):
                     lhsT_scale=xs[:, c, g, 128 * a:128 * a + 128],
                     rhs=wc[:, g, 512 * n:512 * n + 512].bitcast(FP8X4),
                     rhs_scale=ws[:, g, 512 * n:512 * n + 512],
-                    start=(g == 0), stop=(g == NG - 1),
-                )
+                    start=(g == 0), stop=(g == NG - 1))
 
-        def load(pool, view, c, nm):
-            t = pool.tile([P, 2, DIN], BF16, name=nm, tag=nm)
-            nc.sync.dma_start(out=t[:], in_=view[c])
-            return t
-
-        order = [("x", 0), ("w", 0), ("w", 1), ("b", 0), ("x", 1), ("w", 2), ("w", 3),
-                 ("x", 2), ("w", 4), ("w", 5), ("x", 3), ("w", 6), ("w", 7)]
-        loaded = {}
-        for kind, c in order:
-            if kind == "x":
-                loaded[(kind, c)] = load(xin, x_v, c, "xt")
-            elif kind == "w":
-                loaded[(kind, c)] = load(win, w_v, c, "wt")
-            else:
-                nc.sync.dma_start(out=bias_bc[:], in_=bias.partition_broadcast(P))
+        ge = nc.gpsimd
 
         def xn_batch():
             xc2 = sm.tile([P, NT], F32, name="xc2", bufs=1)
-            nc.gpsimd.tensor_scalar(out=xc2[:], in0=xn2[:], scalar1=1e-30, scalar2=None, op0=ALU.max)
+            ge.tensor_tensor(out=xc2[:], in0=xn2[:, 0, :], in1=xn2[:, 1, :], op=ALU.add)
+            ge.tensor_scalar(out=xc2[:], in0=xc2[:], scalar1=1e-30, scalar2=None, op0=ALU.max)
             rxn = sm.tile([P, NT], F32, name="rxn", bufs=1)
-            nc.gpsimd.tensor_tensor(out=rxn[:], in0=xc2[:], in1=mh8[:], op=ALU.pow)
+            ge.tensor_tensor(out=rxn[:], in0=xc2[:], in1=mh8[:], op=ALU.pow)
             v = sm.tile([P, NT], F32, name="v", bufs=1)
-            nc.vector.tensor_tensor(out=v[:], in0=xc2[:], in1=rxn[:], op=ALU.mult)
-            nc.vector.tensor_scalar(out=v[:], in0=v[:], scalar1=1.0 - 1e-5, scalar2=None, op0=ALU.min)
+            ge.tensor_tensor(out=v[:], in0=xc2[:], in1=rxn[:], op=ALU.mult)
+            ge.tensor_scalar(out=v[:], in0=v[:], scalar1=1.0 - 1e-5, scalar2=None, op0=ALU.min)
             l1 = sm.tile([P, NT], F32, name="l1", bufs=1)
             l2 = sm.tile([P, NT], F32, name="l2", bufs=1)
             nc.scalar.activation(out=l1[:], in_=v[:], func=ACT.Ln, bias=1.0, scale=1.0)
             nc.scalar.activation(out=l2[:], in_=v[:], func=ACT.Ln, bias=1.0, scale=-1.0)
-            nc.vector.tensor_tensor(out=l1[:], in0=l1[:], in1=l2[:], op=ALU.subtract)
-            nc.vector.scalar_tensor_tensor(out=q[:], in0=l1[:], scalar=0.5, in1=rxn[:],
-                                           op0=ALU.mult, op1=ALU.mult)
+            d = sm.tile([P, NT], F32, name="d", bufs=1)
+            ge.tensor_tensor(out=d[:], in0=l1[:], in1=l2[:], op=ALU.subtract)
+            ge.tensor_tensor(out=d[:], in0=d[:], in1=rxn[:], op=ALU.mult)
+            ge.tensor_scalar(out=q[:], in0=d[:], scalar1=0.5, scalar2=None, op0=ALU.mult)
 
         def bias_map():
+            jb = sm.tile([P, DOUT // P], F32, name="jb", bufs=1)
             sb = sm.tile([P, 1], F32, name="sb", bufs=1)
-            nc.scalar.activation(out=b_bc[:], in_=bias_bc[:], func=ACT.Square, accum_out=sb[:])
+            nc.scalar.activation(out=jb[:], in_=bias_p[:], func=ACT.Square, accum_out=sb[:])
+            tot = psum.tile([P, 1], F32, tag="bk0", name="tot")
+            nc.tensor.matmul(out=tot[:], lhsT=ones[:], rhs=sb[:], start=True, stop=True)
+            u2s = sm.tile([P, 1], F32, name="u2s", bufs=1)
+            nc.scalar.activation(out=u2s[:], in_=tot[:], func=ACT.Copy, scale=0.01)
             u2 = sm.tile([P, 1], F32, name="u2", bufs=1)
-            nc.gpsimd.tensor_scalar(out=u2[:], in0=sb[:], scalar1=0.01, scalar2=1e-30,
-                                    op0=ALU.mult, op1=ALU.max)
+            ge.tensor_scalar(out=u2[:], in0=u2s[:], scalar1=1e-30, scalar2=None, op0=ALU.max)
             run = sm.tile([P, 1], F32, name="run", bufs=1)
-            nc.gpsimd.tensor_tensor(out=run[:], in0=u2[:], in1=mh8[:, 0:1], op=ALU.pow)
+            ge.tensor_tensor(out=run[:], in0=u2[:], in1=mh8[:, 0:1], op=ALU.pow)
+            return u2, run
+
+        def bias_map2(u2, run):
             tb = sm.tile([P, 1], F32, name="tb", bufs=1)
             nc.scalar.activation(out=tb[:], in_=u2[:], func=ACT.Tanh, scale=run[:, 0:1])
-            scb = sm.tile([P, 1], F32, name="scb", bufs=1)
-            nc.vector.tensor_scalar(out=scb[:], in0=tb[:], scalar1=run[:, 0:1], scalar2=0.1,
-                                    op0=ALU.mult, op1=ALU.mult)
-            nc.vector.tensor_tensor(out=y2[:], in0=tb[:], in1=tb[:], op=ALU.mult)
-            nc.vector.tensor_scalar(out=c2[:], in0=y2[:], scalar1=-1.0, scalar2=None, op0=ALU.add)
-            nc.vector.tensor_scalar(out=b_bc[:], in0=bias_bc[:], scalar1=scb[:, 0:1], scalar2=None,
-                                    op0=ALU.mult)
-
-        for kind, c in order:
-            if kind == "x":
-                x_pair(c, loaded[(kind, c)])
-                if c == 3:
-                    xn_batch()
-                    bias_map()
-            elif kind == "w":
-                w_pair(c, loaded[(kind, c)])
-                if c % 2 == 1:
-                    mx_block(0, c // 2)
+            ge.tensor_scalar(out=scb[:], in0=tb[:], scalar1=run[:, 0:1], scalar2=0.1,
+                             op0=ALU.mult, op1=ALU.mult)
+            ge.tensor_scalar(out=scb2[:], in0=scb[:], scalar1=2.0, scalar2=None, op0=ALU.mult)
+            ge.tensor_tensor(out=y2[:], in0=tb[:], in1=tb[:], op=ALU.mult)
+            ge.tensor_scalar(out=y21[:], in0=y2[:], scalar1=1.0, scalar2=None, op0=ALU.add)
 
         sums = {}
         coef = {}
-        tts = {}
+        zt = {}
 
-        def sums_of(r):
-            ssq = sm.tile([P, NB], F32, name="ssq")
-            dot = sm.tile([P, NB], F32, name="dot")
-            sums[r] = (ssq, dot)
-            for n in range(NB):
-                acc = banks[(r, n)]
-                jk = jkp.tile([P, 512], F32, name="jk", tag="jk")
-                nc.scalar.activation(out=jk[:], in_=acc[:], func=ACT.Square,
-                                     accum_out=ssq[:, n:n + 1])
-                nc.vector.scalar_tensor_tensor(out=jk[:], in0=acc[:], scalar=2.0,
-                                               in1=b_bc[:, 512 * n:512 * n + 512],
-                                               op0=ALU.mult, op1=ALU.mult,
-                                               accum_out=dot[:, n:n + 1])
+        def new_sums(r):
+            sums[r] = (sm.tile([P, NB], F32, name="ssq"), sm.tile([P, NB], F32, name="dot"))
 
-        def col(nm):
-            return sm.tile([P, 1], F32, name=nm, tag=nm)
+        def ssq(r, n):
+            js = jkp.tile([P, 512], F32, name="js", tag="js")
+            nc.scalar.activation(out=js[:], in_=banks[(r, n)][:], func=ACT.Square,
+                                 accum_out=sums[r][0][:, n:n + 1])
 
-        def chain_stages(r):
-            ssq, dot = sums[r]
-            ce = nc.vector
-            loc = {}
+        def dot(r, n):
+            jv = jkp.tile([P, 512], F32, name="jv", tag="jv")
+            nc.vector.scalar_tensor_tensor(out=jv[:], in0=banks[(r, n)][:], scalar=scb2[:, 0:1],
+                                           in1=bias_bc[:, 512 * n:512 * n + 512],
+                                           op0=ALU.mult, op1=ALU.mult,
+                                           accum_out=sums[r][1][:, n:n + 1])
 
-            def st_a():
-                y = col("y")
-                nc.vector.tensor_reduce(out=y[:], in_=ssq[:], axis=AX.X, op=ALU.add)
-                d2 = col("d2")
-                nc.vector.tensor_reduce(out=d2[:], in_=dot[:], axis=AX.X, op=ALU.add)
-                yc = col("yc")
-                nc.gpsimd.tensor_scalar(out=yc[:], in0=y[:], scalar1=1e-30, scalar2=None, op0=ALU.max)
-                rmn = col("rmn")
-                nc.gpsimd.tensor_tensor(out=rmn[:], in0=yc[:], in1=mh8[:, 0:1], op=ALU.pow)
-                sq = col("sq")
-                nc.gpsimd.tensor_scalar(out=sq[:], in0=rmn[:], scalar1=q[:, r:r + 1], scalar2=None,
-                                        op0=ALU.mult)
-                th = col("th")
-                nc.scalar.activation(out=th[:], in_=yc[:], func=ACT.Tanh, scale=sq[:, 0:1])
-                loc["d2"], loc["rmn"], loc["th"] = d2, rmn, th
+        def col(nm, w=1):
+            return sm.tile([P, w], F32, name=nm, tag=nm)
 
-            def st_b():
-                th, rmn, d2 = loc["th"], loc["rmn"], loc["d2"]
-                s = col("s")
-                ce.tensor_scalar(out=s[:], in0=th[:], scalar1=rmn[:, 0:1], scalar2=None, op0=ALU.mult)
-                x2 = col("x2")
-                ce.tensor_scalar(out=x2[:], in0=th[:], scalar1=th[:, 0:1], scalar2=None, op0=ALU.mult)
-                e1 = col("e1")
-                ce.tensor_scalar(out=e1[:], in0=s[:], scalar1=d2[:, 0:1], scalar2=1.0,
-                                 op0=ALU.mult, op1=ALU.add)
-                pk = sm.tile([P, 2], F32, name="pk", tag="pk")
-                den = col("den")
-                ce.tensor_scalar(out=den[:], in0=x2[:], scalar1=y2[:, 0:1], scalar2=e1[:, 0:1],
-                                 op0=ALU.mult, op1=ALU.add)
-                num = col("num")
-                ce.tensor_scalar(out=num[:], in0=x2[:], scalar1=c2[:, 0:1], scalar2=e1[:, 0:1],
-                                 op0=ALU.add, op1=ALU.add)
-                ce.tensor_scalar(out=pk[:, 0:1], in0=den[:], scalar1=1e-15, scalar2=None, op0=ALU.max)
-                ce.tensor_scalar(out=pk[:, 1:2], in0=num[:], scalar1=pk[:, 0:1], scalar2=1e-30,
-                                 op0=ALU.mult, op1=ALU.max)
-                pw = sm.tile([P, 2], F32, name="pw", tag="pw")
-                nc.gpsimd.tensor_tensor(out=pw[:], in0=pk[:], in1=ex2[:], op=ALU.pow)
-                asx = col("asx")
-                ce.tensor_scalar(out=asx[:], in0=e1[:], scalar1=y2[:, 0:1], scalar2=s[:, 0:1],
-                                 op0=ALU.add, op1=ALU.mult)
-                bc = col("bc")
-                ce.tensor_scalar(out=bc[:], in0=x2[:], scalar1=-1.0, scalar2=1.0,
-                                 op0=ALU.mult, op1=ALU.add)
-                loc["pw"], loc["asx"], loc["bc"] = pw, asx, bc
+        def chain_a(r):
+            sq = sums[r][0]
+            h, yc, rmn, v, th = col("h", 2), col("yc"), col("rmn"), col("va"), col("th")
+            s, x2, bc = col("s"), col("x2"), col("bc")
+            coef[r] = {"s": s, "x2": x2, "bc": bc}
+            return [
+                lambda: ge.tensor_tensor(out=h[:], in0=sq[:, 0:2], in1=sq[:, 2:4], op=ALU.add),
+                lambda: ge.tensor_scalar(out=yc[:], in0=h[:, 0:1], scalar1=h[:, 1:2], scalar2=1e-30,
+                                         op0=ALU.add, op1=ALU.max),
+                lambda: ge.tensor_tensor(out=rmn[:], in0=yc[:], in1=mh8[:, 0:1], op=ALU.pow),
+                lambda: ge.tensor_scalar(out=v[:], in0=yc[:], scalar1=q[:, r:r + 1], scalar2=rmn[:, 0:1],
+                                         op0=ALU.mult, op1=ALU.mult),
+                lambda: nc.scalar.activation(out=th[:], in_=v[:], func=ACT.Tanh),
+                lambda: ge.tensor_scalar(out=s[:], in0=th[:], scalar1=rmn[:, 0:1], scalar2=1e-30,
+                                         op0=ALU.mult, op1=ALU.max),
+                lambda: ge.tensor_tensor(out=x2[:], in0=th[:], in1=th[:], op=ALU.mult),
+                lambda: ge.tensor_scalar(out=bc[:], in0=x2[:], scalar1=-1.0, scalar2=1.0,
+                                         op0=ALU.mult, op1=ALU.add),
+            ]
 
-            def st_c():
-                pw, asx, bc = loc["pw"], loc["asx"], loc["bc"]
-                pr = col("pr")
-                ce.tensor_scalar(out=pr[:], in0=pw[:, 1:2], scalar1=0.999, scalar2=pw[:, 0:1],
-                                 op0=ALU.mult, op1=ALU.min)
-                al = col("al")
-                ce.tensor_scalar(out=al[:], in0=asx[:], scalar1=pr[:, 0:1], scalar2=None, op0=ALU.mult)
-                be = col("be")
-                ce.tensor_scalar(out=be[:], in0=bc[:], scalar1=pr[:, 0:1], scalar2=None, op0=ALU.mult)
-                coef[r] = (al, be)
+        def chain_b(r):
+            k = coef[r]
+            dt = sums[r][1]
+            hd, xy, a0, ra, de = col("hd", 2), col("xy"), col("a0"), col("ra"), col("de")
+            k["de"], k["a0"], k["xy"] = de, a0, xy
+            return [
+                lambda: ge.tensor_tensor(out=hd[:], in0=dt[:, 0:2], in1=dt[:, 2:4], op=ALU.add),
+                lambda: ge.tensor_scalar(out=xy[:], in0=hd[:, 0:1], scalar1=hd[:, 1:2],
+                                         scalar2=k["s"][:, 0:1], op0=ALU.add, op1=ALU.mult),
+                lambda: ge.tensor_scalar(out=a0[:], in0=xy[:], scalar1=y21[:, 0:1],
+                                         scalar2=k["s"][:, 0:1], op0=ALU.add, op1=ALU.mult),
+                lambda: ge.tensor_tensor(out=ra[:], in0=a0[:], in1=m1[:], op=ALU.pow),
+                lambda: ge.tensor_scalar(out=de[:], in0=ra[:], scalar1=k["bc"][:, 0:1],
+                                         scalar2=scb[:, 0:1], op0=ALU.mult, op1=ALU.mult),
+            ]
 
-            return [st_a, st_b, st_c]
+        def chain_c(r):
+            k = coef[r]
+            nb, dn, mx, pd, pr, al = (col("nb", 2), col("dn", 2), col("mx"), col("pd"), col("pr"), col("al"))
+            k["al"] = al
+            return [
+                lambda: ge.tensor_scalar(out=nb[:, 0:1], in0=k["x2"][:], scalar1=y2[:, 0:1], scalar2=1.0,
+                                         op0=ALU.mult, op1=ALU.add),
+                lambda: ge.tensor_scalar(out=nb[:, 1:2], in0=k["x2"][:], scalar1=y2[:, 0:1], scalar2=None,
+                                         op0=ALU.add),
+                lambda: ge.tensor_scalar(out=dn[:], in0=nb[:], scalar1=k["xy"][:, 0:1], scalar2=None,
+                                         op0=ALU.add),
+                lambda: ge.tensor_scalar(out=mx[:], in0=dn[:, 1:2], scalar1=1.0 / (0.999 * 0.999),
+                                         scalar2=dn[:, 0:1], op0=ALU.mult, op1=ALU.max),
+                lambda: ge.tensor_scalar(out=pd[:], in0=mx[:], scalar1=dn[:, 0:1], scalar2=1e-30,
+                                         op0=ALU.mult, op1=ALU.max),
+                lambda: ge.tensor_tensor(out=pr[:], in0=pd[:], in1=mh8[:, 0:1], op=ALU.pow),
+                lambda: ge.tensor_tensor(out=al[:], in0=k["a0"][:], in1=pr[:], op=ALU.mult),
+            ]
 
-        def scale_rows(r):
-            al, be = coef[r]
-            t = tpl.tile([P, DOUT], F32, name="t", tag="t")
-            tts[r] = t
-            for n in range(NB):
-                nc.scalar.activation(out=t[:, 512 * n:512 * n + 512], in_=banks[(r, n)][:],
-                                     func=ACT.Copy, scale=al[:, 0:1])
+        def run_all(steps):
+            for st in steps:
+                st()
 
-        def add_bias(r, h):
-            al, be = coef[r]
-            t = tts[r]
+        def zip_run(a, b):
+            for i in range(max(len(a), len(b))):
+                if i < len(a):
+                    a[i]()
+                if i < len(b):
+                    b[i]()
+
+        def zrow(r, n):
+            if n == 0:
+                zt[r] = zp.tile([P, DOUT], F32, name="z", tag="z")
+            sl = slice(512 * n, 512 * n + 512)
+            nc.vector.scalar_tensor_tensor(out=zt[r][:, sl], in0=bias_bc[:, sl], scalar=coef[r]["de"][:, 0:1],
+                                           in1=banks[(r, n)][:], op0=ALU.mult, op1=ALU.add)
+
+        def leaky(r, h):
             sl = slice(1024 * h, 1024 * h + 1024)
-            nc.vector.scalar_tensor_tensor(out=t[:, sl], in0=b_bc[:, sl], scalar=be[:, 0:1],
-                                           in1=t[:, sl], op0=ALU.mult, op1=ALU.add)
+            z = zt[r]
+            nc.vector.scalar_tensor_tensor(out=z[:, sl], in0=z[:, sl], scalar=0.2,
+                                           in1=z[:, sl], op0=ALU.mult, op1=ALU.max)
 
-        def leaky_store(r, h):
-            t = tts[r]
+        def scale_store(r, h):
             sl = slice(1024 * h, 1024 * h + 1024)
-            nc.vector.scalar_tensor_tensor(out=t[:, sl], in0=t[:, sl], scalar=0.2,
-                                           in1=t[:, sl], op0=ALU.mult, op1=ALU.max)
-            nc.sync.dma_start(out=out_v[r][:, sl], in_=t[:, sl])
+            z = zt[r]
+            nc.scalar.activation(out=z[:, sl], in_=z[:, sl], func=ACT.Copy, scale=coef[r]["al"][:, 0:1])
+            nc.sync.dma_start(out=out_v[r][:, sl], in_=z[:, sl])
 
-        for r in range(NT + 1):
-            if r < NT:
-                if r > 0:
-                    for n in range(NB):
-                        mx_block(r, n)
-                sums_of(r)
-            stages = chain_stages(r) if r < NT else []
-            if r > 0:
-                scale_rows(r - 1)
-            big = []
-            if r > 0:
-                big = [lambda: add_bias(r - 1, 0), lambda: add_bias(r - 1, 1),
-                       lambda: leaky_store(r - 1, 0), lambda: leaky_store(r - 1, 1)]
-            for i in range(4):
-                if i < len(stages):
-                    stages[i]()
-                if i < len(big):
-                    big[i]()
+        n_pairs = len(ORDER)
+        norms = []
+        new_sums(0)
+        pending_mm = []
+        pending_dot = []
+        for i in range(AHEAD):
+            load(i)
+            if i == 0:
+                nc.sync.dma_start(out=bias_p[:], in_=bias.rearrange("(p j) -> p j", p=P))
+            if i == 2:
+                nc.sync.dma_start(out=bias_bc[:], in_=bias.partition_broadcast(P))
+        premult(0)
+        for i in range(n_pairs):
+            if i + AHEAD < n_pairs:
+                load(i + AHEAD)
+            for n in pending_dot:
+                ssq(0, n)
+            if i >= 1:
+                quantise(i - 1)
+            if i + 1 < n_pairs:
+                premult(i + 1)
+            transpose_and_copy(i)
+            if i == 1:
+                bm = bias_map()
+            if i == 2:
+                bias_map2(*bm)
+            for n in pending_mm:
+                mx_block(0, n)
+            for n in pending_dot:
+                dot(0, n)
+            pending_dot = pending_mm
+            pending_mm = []
+            if i >= 1:
+                kind, c = ORDER[i - 1]
+                if kind == "w" and c % 2 == 1:
+                    pending_mm = [c // 2]
+            if ORDER[i][0] == "x":
+                norms += [(i, 0, 0), (i, 0, 1), (i, 1, 0), (i, 1, 1)]
+            for j in range(2):
+                if norms:
+                    x_norm(*norms.pop(0))
+        for nm in norms:
+            x_norm(*nm)
+        xn_batch()
+        quantise(n_pairs - 1)
+        for n in pending_dot:
+            ssq(0, n)
+            dot(0, n)
+        for n in pending_mm:
+            mx_block(0, n)
+            ssq(0, n)
+            dot(0, n)
+        mx_block(0, NB - 1)
+        ssq(0, NB - 1)
+        dot(0, NB - 1)
+        new_sums(1)
+        ca = chain_a(0)
+        run_all(ca[:4])
+        for n in range(NB):
+            mx_block(1, n)
+            ssq(1, n)
+            if n == 1:
+                run_all(ca[4:])
+                run_all(chain_b(0))
+        zip_run(chain_a(1), chain_c(0))
+
+        for r in range(NT):
+            if r + 1 < NT:
+                for n in range(NB):
+                    dot(r + 1, n)
+                run_all(chain_b(r + 1))
+            for n in range(NB):
+                zrow(r, n)
+            cc = chain_c(r + 1) if r + 1 < NT else []
+            if r + 2 < NT:
+                new_sums(r + 2)
+                for n in range(NB):
+                    mx_block(r + 2, n)
+                    ssq(r + 2, n)
+            leaky(r, 0)
+            leaky(r, 1)
+            scale_store(r, 0)
+            scale_store(r, 1)
+            ca = chain_a(r + 2) if r + 2 < NT else []
+            zip_run(ca, cc)

@@ -47,8 +47,8 @@ def tile_hypequalizedlinear_kernel(tc, x, weight, bias, out):
         make_identity(nc, ident[:])
         mh8 = const.tile([P, NT], F32, name="mh8")
         nc.gpsimd.memset(mh8[:], -0.5)
-        m1 = const.tile([P, 1], F32, name="m1")
-        nc.gpsimd.memset(m1[:], -1.0)
+        tiny = const.tile([P, 1], F32, name="tiny")
+        nc.gpsimd.memset(tiny[:], 2.0 ** -102)
         ones = const.tile([P, P], F32, name="ones")
         nc.gpsimd.memset(ones[:], 1.0)
 
@@ -61,9 +61,8 @@ def tile_hypequalizedlinear_kernel(tc, x, weight, bias, out):
         xn2 = const.tile([P, 2, NT], F32, name="xn2")
         q = const.tile([P, NT], F32, name="q")
         y2 = const.tile([P, 1], F32, name="y2")
-        y21 = const.tile([P, 1], F32, name="y21")
-        scb = const.tile([P, 1], F32, name="scb")
-        scb2 = const.tile([P, 1], F32, name="scb2")
+        nscb = const.tile([P, 1], F32, name="nscb")
+        ny4 = const.tile([P, 1], F32, name="ny4")
 
         raw = {}
 
@@ -183,11 +182,14 @@ def tile_hypequalizedlinear_kernel(tc, x, weight, bias, out):
         def bias_map2(u2, run):
             tb = sm.tile([P, 1], F32, name="tb", bufs=1)
             nc.scalar.activation(out=tb[:], in_=u2[:], func=ACT.Tanh, scale=run[:, 0:1])
-            ge.tensor_scalar(out=scb[:], in0=tb[:], scalar1=run[:, 0:1], scalar2=0.1,
+            ge.tensor_scalar(out=nscb[:], in0=tb[:], scalar1=run[:, 0:1], scalar2=-0.1,
                              op0=ALU.mult, op1=ALU.mult)
-            ge.tensor_scalar(out=scb2[:], in0=scb[:], scalar1=2.0, scalar2=None, op0=ALU.mult)
             ge.tensor_tensor(out=y2[:], in0=tb[:], in1=tb[:], op=ALU.mult)
-            ge.tensor_scalar(out=y21[:], in0=y2[:], scalar1=1.0, scalar2=None, op0=ALU.add)
+            rnb = sm.tile([P, 1], F32, name="rnb", bufs=1)
+            nc.vector.reciprocal(out=rnb[:], in_=nscb[:])
+            y4 = sm.tile([P, 1], F32, name="y4", bufs=1)
+            ge.tensor_scalar(out=y4[:], in0=y2[:], scalar1=1.0, scalar2=0.25, op0=ALU.add, op1=ALU.mult)
+            ge.tensor_tensor(out=ny4[:], in0=y4[:], in1=rnb[:], op=ALU.mult)
 
         sums = {}
         coef = {}
@@ -203,7 +205,7 @@ def tile_hypequalizedlinear_kernel(tc, x, weight, bias, out):
 
         def dot(r, n):
             jv = jkp.tile([P, 512], F32, name="jv", tag="jv")
-            nc.vector.scalar_tensor_tensor(out=jv[:], in0=banks[(r, n)][:], scalar=scb2[:, 0:1],
+            nc.vector.scalar_tensor_tensor(out=jv[:], in0=banks[(r, n)][:], scalar=-2.0,
                                            in1=bias_bc[:, 512 * n:512 * n + 512],
                                            op0=ALU.mult, op1=ALU.mult,
                                            accum_out=sums[r][1][:, n:n + 1])
@@ -212,77 +214,82 @@ def tile_hypequalizedlinear_kernel(tc, x, weight, bias, out):
             return sm.tile([P, w], F32, name=nm, tag=nm)
 
         def chain_a(r):
-            sq = sums[r][0]
-            h, yc, rmn, v, th = col("h", 2), col("yc"), col("rmn"), col("va"), col("th")
-            s, x2, bc = col("s"), col("x2"), col("bc")
-            coef[r] = {"s": s, "x2": x2, "bc": bc}
-            return [
-                lambda: ge.tensor_tensor(out=h[:], in0=sq[:, 0:2], in1=sq[:, 2:4], op=ALU.add),
-                lambda: ge.tensor_scalar(out=yc[:], in0=h[:, 0:1], scalar1=h[:, 1:2], scalar2=1e-30,
-                                         op0=ALU.add, op1=ALU.max),
-                lambda: ge.tensor_tensor(out=rmn[:], in0=yc[:], in1=mh8[:, 0:1], op=ALU.pow),
-                lambda: ge.tensor_scalar(out=v[:], in0=yc[:], scalar1=q[:, r:r + 1], scalar2=rmn[:, 0:1],
-                                         op0=ALU.mult, op1=ALU.mult),
-                lambda: nc.scalar.activation(out=th[:], in_=v[:], func=ACT.Tanh),
-                lambda: ge.tensor_scalar(out=s[:], in0=th[:], scalar1=rmn[:, 0:1], scalar2=1e-30,
-                                         op0=ALU.mult, op1=ALU.max),
-                lambda: ge.tensor_tensor(out=x2[:], in0=th[:], in1=th[:], op=ALU.mult),
-                lambda: ge.tensor_scalar(out=bc[:], in0=x2[:], scalar1=-1.0, scalar2=1.0,
-                                         op0=ALU.mult, op1=ALU.add),
-            ]
+            y, yq, rmn = col("y"), col("yq"), col("rmn")
+            coef[r] = {"yq": yq, "rmn": rmn}
+            j4 = col("j4", NB)
+            nc.scalar.activation(out=j4[:], in_=sums[r][0][:], func=ACT.Identity, bias=tiny[:, 0:1],
+                                 accum_out=y[:])
+            nc.scalar.activation(out=yq[:], in_=y[:], func=ACT.Copy, scale=q[:, r:r + 1])
+            ge.tensor_tensor(out=rmn[:], in0=y[:], in1=mh8[:, 0:1], op=ALU.pow)
 
-        def chain_b(r):
+        def chain_t(r):
             k = coef[r]
+            th, x2 = col("th"), col("x2")
+            k["th"], k["x2"] = th, x2
+            nc.scalar.activation(out=th[:], in_=k["yq"][:], func=ACT.Tanh, scale=k["rmn"][:, 0:1])
+            nc.scalar.activation(out=x2[:], in_=th[:], func=ACT.Square)
+
+        def chain_v1(r):
+            k = coef[r]
+            k["nbc"] = col("nbc")
+            nc.vector.tensor_scalar(out=k["nbc"][:], in0=k["x2"][:], scalar1=1.0, scalar2=-1e-18,
+                                    op0=ALU.subtract, op1=ALU.min)
+
+        def chain_v2(r):
+            k = coef[r]
+            k["rn"] = col("rn")
+            nc.vector.reciprocal(out=k["rn"][:], in_=k["nbc"][:])
+
+        def chain_s(r):
+            k = coef[r]
+            s, w, sw, yw = col("s"), col("w"), col("sw"), col("yw")
+            k["s"], k["sw"], k["yw"] = s, sw, yw
+            nc.scalar.activation(out=s[:], in_=k["th"][:], func=ACT.Copy, scale=k["rmn"][:, 0:1])
+            nc.scalar.activation(out=w[:], in_=s[:], func=ACT.Copy, scale=k["rn"][:, 0:1])
+            nc.scalar.activation(out=sw[:], in_=s[:], func=ACT.Copy, scale=w[:, 0:1])
+            nc.scalar.activation(out=yw[:], in_=w[:], func=ACT.Copy, scale=ny4[:, 0:1])
+
+        def chain_g(r):
+            k = coef[r]
+            ga = col("ga")
+            k["ga"] = ga
+            j4 = col("j4", NB)
+            nc.scalar.activation(out=j4[:], in_=sums[r][1][:], func=ACT.Identity, scale=k["sw"][:, 0:1],
+                                 bias=k["yw"][:, 0:1], accum_out=ga[:])
+
+        def chain_c1(r):
+            k = coef[r]
+            xs, nb, hd, xy, dn = col("xs"), col("nb", 2), col("hd", 2), col("xy"), col("dn", 2)
+            k["dn"] = dn
             dt = sums[r][1]
-            hd, xy, a0, ra, de = col("hd", 2), col("xy"), col("a0"), col("ra"), col("de")
-            k["de"], k["a0"], k["xy"] = de, a0, xy
-            return [
-                lambda: ge.tensor_tensor(out=hd[:], in0=dt[:, 0:2], in1=dt[:, 2:4], op=ALU.add),
-                lambda: ge.tensor_scalar(out=xy[:], in0=hd[:, 0:1], scalar1=hd[:, 1:2],
-                                         scalar2=k["s"][:, 0:1], op0=ALU.add, op1=ALU.mult),
-                lambda: ge.tensor_scalar(out=a0[:], in0=xy[:], scalar1=y21[:, 0:1],
-                                         scalar2=k["s"][:, 0:1], op0=ALU.add, op1=ALU.mult),
-                lambda: ge.tensor_tensor(out=ra[:], in0=a0[:], in1=m1[:], op=ALU.pow),
-                lambda: ge.tensor_scalar(out=de[:], in0=ra[:], scalar1=k["bc"][:, 0:1],
-                                         scalar2=scb[:, 0:1], op0=ALU.mult, op1=ALU.mult),
-            ]
+            ge.tensor_tensor(out=hd[:], in0=dt[:, 0:2], in1=dt[:, 2:4], op=ALU.add)
+            ge.tensor_tensor(out=xs[:], in0=k["s"][:], in1=nscb[:], op=ALU.mult)
+            ge.tensor_scalar(out=nb[:, 0:1], in0=k["x2"][:], scalar1=y2[:, 0:1], scalar2=1.0,
+                             op0=ALU.mult, op1=ALU.add)
+            ge.tensor_scalar(out=nb[:, 1:2], in0=k["x2"][:], scalar1=y2[:, 0:1], scalar2=None, op0=ALU.add)
+            ge.tensor_scalar(out=xy[:], in0=hd[:, 0:1], scalar1=hd[:, 1:2], scalar2=xs[:, 0:1],
+                             op0=ALU.add, op1=ALU.mult)
+            ge.tensor_scalar(out=dn[:], in0=nb[:], scalar1=xy[:, 0:1], scalar2=None, op0=ALU.add)
 
-        def chain_c(r):
+        def chain_c2(r):
             k = coef[r]
-            nb, dn, mx, pd, pr, al = (col("nb", 2), col("dn", 2), col("mx"), col("pd"), col("pr"), col("al"))
-            k["al"] = al
-            return [
-                lambda: ge.tensor_scalar(out=nb[:, 0:1], in0=k["x2"][:], scalar1=y2[:, 0:1], scalar2=1.0,
-                                         op0=ALU.mult, op1=ALU.add),
-                lambda: ge.tensor_scalar(out=nb[:, 1:2], in0=k["x2"][:], scalar1=y2[:, 0:1], scalar2=None,
-                                         op0=ALU.add),
-                lambda: ge.tensor_scalar(out=dn[:], in0=nb[:], scalar1=k["xy"][:, 0:1], scalar2=None,
-                                         op0=ALU.add),
-                lambda: ge.tensor_scalar(out=mx[:], in0=dn[:, 1:2], scalar1=1.0 / (0.999 * 0.999),
-                                         scalar2=dn[:, 0:1], op0=ALU.mult, op1=ALU.max),
-                lambda: ge.tensor_scalar(out=pd[:], in0=mx[:], scalar1=dn[:, 0:1], scalar2=1e-30,
-                                         op0=ALU.mult, op1=ALU.max),
-                lambda: ge.tensor_tensor(out=pr[:], in0=pd[:], in1=mh8[:, 0:1], op=ALU.pow),
-                lambda: ge.tensor_tensor(out=al[:], in0=k["a0"][:], in1=pr[:], op=ALU.mult),
-            ]
-
-        def run_all(steps):
-            for st in steps:
-                st()
-
-        def zip_run(a, b):
-            for i in range(max(len(a), len(b))):
-                if i < len(a):
-                    a[i]()
-                if i < len(b):
-                    b[i]()
+            mx, pd, pr, be = col("mx"), col("pd"), col("pr"), col("be")
+            k["be"] = be
+            dn = k["dn"]
+            ge.tensor_scalar(out=mx[:], in0=dn[:, 1:2], scalar1=1.0 / (0.999 * 0.999),
+                             scalar2=dn[:, 0:1], op0=ALU.mult, op1=ALU.max)
+            ge.tensor_scalar(out=pd[:], in0=mx[:], scalar1=dn[:, 0:1], scalar2=1e-30,
+                             op0=ALU.mult, op1=ALU.max)
+            ge.tensor_tensor(out=pr[:], in0=pd[:], in1=mh8[:, 0:1], op=ALU.pow)
+            ge.tensor_scalar(out=be[:], in0=pr[:], scalar1=k["nbc"][:, 0:1], scalar2=nscb[:, 0:1],
+                             op0=ALU.mult, op1=ALU.mult)
 
         def zrow(r, n):
             if n == 0:
                 zt[r] = zp.tile([P, DOUT], F32, name="z", tag="z")
             sl = slice(512 * n, 512 * n + 512)
-            nc.vector.scalar_tensor_tensor(out=zt[r][:, sl], in0=bias_bc[:, sl], scalar=coef[r]["de"][:, 0:1],
-                                           in1=banks[(r, n)][:], op0=ALU.mult, op1=ALU.add)
+            nc.vector.scalar_tensor_tensor(out=zt[r][:, sl], in0=banks[(r, n)][:], scalar=coef[r]["ga"][:, 0:1],
+                                           in1=bias_bc[:, sl], op0=ALU.mult, op1=ALU.add)
 
         def leaky(r, h):
             sl = slice(1024 * h, 1024 * h + 1024)
@@ -293,7 +300,7 @@ def tile_hypequalizedlinear_kernel(tc, x, weight, bias, out):
         def scale_store(r, h):
             sl = slice(1024 * h, 1024 * h + 1024)
             z = zt[r]
-            nc.scalar.activation(out=z[:, sl], in_=z[:, sl], func=ACT.Copy, scale=coef[r]["al"][:, 0:1])
+            nc.scalar.activation(out=z[:, sl], in_=z[:, sl], func=ACT.Copy, scale=coef[r]["be"][:, 0:1])
             nc.sync.dma_start(out=out_v[r][:, sl], in_=z[:, sl])
 
         n_pairs = len(ORDER)
@@ -351,33 +358,50 @@ def tile_hypequalizedlinear_kernel(tc, x, weight, bias, out):
         mx_block(0, NB - 1)
         ssq(0, NB - 1)
         dot(0, NB - 1)
+        chain_a(0)
         new_sums(1)
-        ca = chain_a(0)
-        run_all(ca[:4])
         for n in range(NB):
             mx_block(1, n)
             ssq(1, n)
             if n == 1:
-                run_all(ca[4:])
-                run_all(chain_b(0))
-        zip_run(chain_a(1), chain_c(0))
+                chain_t(0)
+                chain_v1(0)
+            dot(1, n)
+            if n == 1:
+                chain_v2(0)
+                chain_s(0)
+                chain_g(0)
+                chain_c1(0)
+        chain_a(1)
+        chain_c2(0)
+        chain_t(1)
 
         for r in range(NT):
-            if r + 1 < NT:
+            if 1 <= r < NT - 1:
                 for n in range(NB):
                     dot(r + 1, n)
-                run_all(chain_b(r + 1))
             for n in range(NB):
                 zrow(r, n)
-            cc = chain_c(r + 1) if r + 1 < NT else []
+                if r + 1 < NT:
+                    if n == 1:
+                        chain_v1(r + 1)
+                    if n == 2:
+                        chain_v2(r + 1)
+            if r + 1 < NT:
+                chain_s(r + 1)
+                chain_g(r + 1)
+                chain_c1(r + 1)
             if r + 2 < NT:
                 new_sums(r + 2)
                 for n in range(NB):
                     mx_block(r + 2, n)
                     ssq(r + 2, n)
+                chain_a(r + 2)
+            if r + 1 < NT:
+                chain_c2(r + 1)
             leaky(r, 0)
-            leaky(r, 1)
             scale_store(r, 0)
+            if r + 2 < NT:
+                chain_t(r + 2)
+            leaky(r, 1)
             scale_store(r, 1)
-            ca = chain_a(r + 2) if r + 2 < NT else []
-            zip_run(ca, cc)

@@ -20,9 +20,17 @@ NG = DIN // 512
 NT = B // P
 NB = DOUT // 512
 
-ORDER = [("x", 0), ("w", 0), ("w", 1), ("x", 1), ("w", 2), ("x", 2), ("w", 3), ("x", 3),
-         ("w", 4), ("w", 5), ("w", 6), ("w", 7)]
-V_GROUPS = [3, 3, 3, 3, 3, 2, 2, 2]
+ORDER = [(s[0], int(s[1])) for s in "w0 w1 x0 w2 w3 x1 w4 w5 x2 w6 w7 x3".split()]
+W_PAT = ["VVVP"] * 5 + ["VVPP"] * 3
+X_PAT = ["SSSS", "SSSS", "SSSS", "VSVV"]
+T_BANKS = [4, 5, 6, 7, 2, 3]
+EARLY = 2
+NORM_RATE = [0, 0, 0, 1, 1, 1, 1, 1, 1, 2, 0, 0]
+LOADS = [(s[0], int(s[1])) for s in "w0 w1 x0 w2 w3 x1 w4 x3 w5 x2 w6 w7".split()]
+GRAM = (1, 2)
+XN_AT = 10
+LAG = 2
+BIAS_AT = 4
 AHEAD = 5
 
 
@@ -36,7 +44,7 @@ def tile_hypequalizedlinear_kernel(tc, x, weight, bias, out):
         const = ctx.enter_context(tc.tile_pool(name="const", bufs=1))
         xin = ctx.enter_context(tc.tile_pool(name="xin", bufs=4))
         win = ctx.enter_context(tc.tile_pool(name="win", bufs=5))
-        gp = ctx.enter_context(tc.tile_pool(name="gp", bufs=3))
+        gp = ctx.enter_context(tc.tile_pool(name="gp", bufs=4))
         zp = ctx.enter_context(tc.tile_pool(name="zp", bufs=3))
         jkp = ctx.enter_context(tc.tile_pool(name="jkp", bufs=2))
         sm = ctx.enter_context(tc.tile_pool(name="sm", bufs=4))
@@ -47,6 +55,8 @@ def tile_hypequalizedlinear_kernel(tc, x, weight, bias, out):
         make_identity(nc, ident[:])
         mh8 = const.tile([P, NT], F32, name="mh8")
         nc.gpsimd.memset(mh8[:], -0.5)
+        m1 = const.tile([P, 1], F32, name="m1")
+        nc.gpsimd.memset(m1[:], -1.0)
         tiny = const.tile([P, 1], F32, name="tiny")
         nc.gpsimd.memset(tiny[:], 2.0 ** -102)
         ones = const.tile([P, P], F32, name="ones")
@@ -60,6 +70,7 @@ def tile_hypequalizedlinear_kernel(tc, x, weight, bias, out):
         ws = const.tile([P, NG, DOUT], U8, name="ws", align_bytes=64)
         xn2 = const.tile([P, 2, NT], F32, name="xn2")
         q = const.tile([P, NT], F32, name="q")
+        nc.gpsimd.memset(xn2[:], 0.0)
         y2 = const.tile([P, 1], F32, name="y2")
         nscb = const.tile([P, 1], F32, name="nscb")
         ny4 = const.tile([P, 1], F32, name="ny4")
@@ -67,11 +78,11 @@ def tile_hypequalizedlinear_kernel(tc, x, weight, bias, out):
         raw = {}
 
         def load(i):
-            kind, c = ORDER[i]
+            kind, c = LOADS[i]
             view = x_v if kind == "x" else w_v
             pool = xin if kind == "x" else win
             t = pool.tile([P, 2, DIN], BF16, name="raw_" + kind, tag="raw_" + kind)
-            raw[i] = t
+            raw[LOADS[i]] = t
             if i < 2:
                 for h in range(2):
                     sl = slice(1024 * h, 1024 * h + 1024)
@@ -81,33 +92,42 @@ def tile_hypequalizedlinear_kernel(tc, x, weight, bias, out):
 
         grouped = {}
 
+        turn = {"n": 0}
+
         def premult(i):
             kind, c = ORDER[i]
             if kind == "w":
-                lo = 512 * V_GROUPS[c]
-                if lo < DIN:
-                    nc.vector.tensor_scalar(out=raw[i][:, :, lo:], in0=raw[i][:, :, lo:], scalar1=0.1,
-                                            scalar2=None, op0=ALU.mult)
+                for g in range(NG):
+                    if W_PAT[c][g] == "P":
+                        sl = slice(512 * g, 512 * g + 512)
+                        nc.vector.tensor_scalar(out=raw[ORDER[i]][:, :, sl], in0=raw[ORDER[i]][:, :, sl], scalar1=0.1,
+                                                scalar2=None, op0=ALU.mult)
 
         def transpose_and_copy(i):
             kind, c = ORDER[i]
-            words = raw[i][:].bitcast(F32)
+            words = raw[ORDER[i]][:].bitcast(F32)
             gt = gp.tile([P, NG, 256, 4], BF16, name="gt", align_bytes=64)
             grouped[i] = gt
             for g in range(NG):
-                tp = psum.tile([P, 2, 2, P], F32, tag="bk%d" % (4 + g), name="tp")
+                tp = psum.tile([P, 2, 2, P], F32, tag="bk%d" % T_BANKS[turn["n"] % len(T_BANKS)], name="tp")
+                turn["n"] += 1
                 for u in range(2):
                     for a in range(2):
                         nc.tensor.transpose(tp[:, u, a, :], words[:, a, 256 * g + u:256 * g + 256:2],
                                             ident[:])
-                if kind == "w" and g < V_GROUPS[c]:
-                    nc.vector.tensor_scalar(
-                        out=gt[:, g, :, :].rearrange("p j (u e) -> p j u e", e=2),
-                        in0=tp[:].bitcast(BF16).rearrange("p u a (r e) -> p (a r) u e", e=2),
-                        scalar1=0.1, scalar2=None, op0=ALU.mult)
+                who = X_PAT[c][g] if kind == "x" else W_PAT[c][g]
+                fout = gt[:, g, :, :].rearrange("p j (u e) -> p j u e", e=2)
+                fin = tp[:].bitcast(BF16).rearrange("p u a (r e) -> p (a r) u e", e=2)
+                wout = gt[:, g, :, :].bitcast(F32)
+                win_ = tp[:].rearrange("p u a r -> p (a r) u")
+                if kind == "w" and who == "V":
+                    nc.vector.tensor_scalar(out=fout, in0=fin, scalar1=0.1, scalar2=None, op0=ALU.mult)
+                elif kind == "w" and who == "S":
+                    nc.scalar.activation(out=fout, in_=fin, func=ACT.Copy, scale=0.1)
+                elif who == "V":
+                    nc.vector.tensor_copy(out=wout, in_=win_)
                 else:
-                    nc.scalar.copy(out=gt[:, g, :, :].bitcast(F32),
-                                   in_=tp[:].rearrange("p u a r -> p (a r) u"))
+                    nc.scalar.copy(out=wout, in_=win_)
 
         def quantise(i):
             kind, c = ORDER[i]
@@ -124,11 +144,29 @@ def tile_hypequalizedlinear_kernel(tc, x, weight, bias, out):
                         scales=ws[:, g, 256 * c:256 * c + 256],
                         in_=gt[:, g, :, :].rearrange("p j t -> p (j t)"))
 
-        def x_norm(i, a, h):
-            c = ORDER[i][1]
+        def x_norm(c, a, h):
             jx = jkp.tile([P, 1024], BF16, name="jx", tag="jx")
-            nc.scalar.activation(out=jx[:], in_=raw[i][:, a, 1024 * h:1024 * h + 1024], func=ACT.Square,
+            nc.scalar.activation(out=jx[:], in_=raw[("x", c)][:, a, 1024 * h:1024 * h + 1024], func=ACT.Square,
                                  accum_out=xn2[:, h, 2 * c + a:2 * c + a + 1])
+
+        gram_t = {}
+
+        def gram(i):
+            gt = grouped[i]
+            gr = psum.tile([P, 2, P], F32, tag="bk3", name="gr")
+            gram_t[i] = gr
+            for a in range(2):
+                for g in range(NG):
+                    for j in range(4):
+                        v = gt[:, g, 128 * a:128 * a + 128, j]
+                        nc.tensor.matmul(out=gr[:, a, :], lhsT=v, rhs=v, start=(g == 0 and j == 0),
+                                         stop=(g == NG - 1 and j == 3))
+
+        def diagonal(i, a):
+            r = 2 * ORDER[i][1] + a
+            jd = jkp.tile([P, P], F32, name="jd", tag="jd")
+            nc.vector.scalar_tensor_tensor(out=jd[:], in0=gram_t[i][:, a, :], scalar=1.0, in1=ident[:],
+                                           op0=ALU.mult, op1=ALU.mult, accum_out=xn2[:, 0, r:r + 1])
 
         banks = {}
 
@@ -147,7 +185,9 @@ def tile_hypequalizedlinear_kernel(tc, x, weight, bias, out):
 
         ge = nc.gpsimd
 
-        def xn_batch():
+        xnt = {}
+
+        def xn_batch1():
             xc2 = sm.tile([P, NT], F32, name="xc2", bufs=1)
             ge.tensor_tensor(out=xc2[:], in0=xn2[:, 0, :], in1=xn2[:, 1, :], op=ALU.add)
             ge.tensor_scalar(out=xc2[:], in0=xc2[:], scalar1=1e-30, scalar2=None, op0=ALU.max)
@@ -156,6 +196,10 @@ def tile_hypequalizedlinear_kernel(tc, x, weight, bias, out):
             v = sm.tile([P, NT], F32, name="v", bufs=1)
             ge.tensor_tensor(out=v[:], in0=xc2[:], in1=rxn[:], op=ALU.mult)
             ge.tensor_scalar(out=v[:], in0=v[:], scalar1=1.0 - 1e-5, scalar2=None, op0=ALU.min)
+            xnt["v"], xnt["rxn"] = v, rxn
+
+        def xn_batch2():
+            v, rxn = xnt["v"], xnt["rxn"]
             l1 = sm.tile([P, NT], F32, name="l1", bufs=1)
             l2 = sm.tile([P, NT], F32, name="l2", bufs=1)
             nc.scalar.activation(out=l1[:], in_=v[:], func=ACT.Ln, bias=1.0, scale=1.0)
@@ -164,6 +208,8 @@ def tile_hypequalizedlinear_kernel(tc, x, weight, bias, out):
             ge.tensor_tensor(out=d[:], in0=l1[:], in1=l2[:], op=ALU.subtract)
             ge.tensor_tensor(out=d[:], in0=d[:], in1=rxn[:], op=ALU.mult)
             ge.tensor_scalar(out=q[:], in0=d[:], scalar1=0.5, scalar2=None, op0=ALU.mult)
+            warm = sm.tile([P, 1], F32, name="warm", bufs=1)
+            nc.scalar.activation(out=warm[:], in_=y2[:], func=ACT.Tanh)
 
         def bias_map():
             jb = sm.tile([P, DOUT // P], F32, name="jb", bufs=1)
@@ -186,9 +232,11 @@ def tile_hypequalizedlinear_kernel(tc, x, weight, bias, out):
                              op0=ALU.mult, op1=ALU.mult)
             ge.tensor_tensor(out=y2[:], in0=tb[:], in1=tb[:], op=ALU.mult)
             rnb = sm.tile([P, 1], F32, name="rnb", bufs=1)
-            nc.vector.reciprocal(out=rnb[:], in_=nscb[:])
+            nb2 = sm.tile([P, 1], F32, name="nb2", bufs=1)
+            ge.tensor_scalar(out=nb2[:], in0=nscb[:], scalar1=-1.0, scalar2=None, op0=ALU.mult)
+            ge.tensor_tensor(out=rnb[:], in0=nb2[:], in1=m1[:], op=ALU.pow)
             y4 = sm.tile([P, 1], F32, name="y4", bufs=1)
-            ge.tensor_scalar(out=y4[:], in0=y2[:], scalar1=1.0, scalar2=0.25, op0=ALU.add, op1=ALU.mult)
+            ge.tensor_scalar(out=y4[:], in0=y2[:], scalar1=1.0, scalar2=-0.25, op0=ALU.add, op1=ALU.mult)
             ge.tensor_tensor(out=ny4[:], in0=y4[:], in1=rnb[:], op=ALU.mult)
 
         sums = {}
@@ -291,20 +339,20 @@ def tile_hypequalizedlinear_kernel(tc, x, weight, bias, out):
             nc.vector.scalar_tensor_tensor(out=zt[r][:, sl], in0=banks[(r, n)][:], scalar=coef[r]["ga"][:, 0:1],
                                            in1=bias_bc[:, sl], op0=ALU.mult, op1=ALU.add)
 
-        def leaky(r, h):
-            sl = slice(1024 * h, 1024 * h + 1024)
+        def leaky(r, n, k):
+            sl = slice(512 * n, 512 * (n + k))
             z = zt[r]
             nc.vector.scalar_tensor_tensor(out=z[:, sl], in0=z[:, sl], scalar=0.2,
                                            in1=z[:, sl], op0=ALU.mult, op1=ALU.max)
 
-        def scale_store(r, h):
-            sl = slice(1024 * h, 1024 * h + 1024)
+        def scale_store(r, n, k):
+            sl = slice(512 * n, 512 * (n + k))
             z = zt[r]
             nc.scalar.activation(out=z[:, sl], in_=z[:, sl], func=ACT.Copy, scale=coef[r]["be"][:, 0:1])
             nc.sync.dma_start(out=out_v[r][:, sl], in_=z[:, sl])
 
         n_pairs = len(ORDER)
-        norms = []
+        norms = [(c, a, h) for c in range(4) if c not in GRAM for a in range(2) for h in range(2)]
         new_sums(0)
         pending_mm = []
         pending_dot = []
@@ -312,54 +360,60 @@ def tile_hypequalizedlinear_kernel(tc, x, weight, bias, out):
             load(i)
             if i == 0:
                 nc.sync.dma_start(out=bias_p[:], in_=bias.rearrange("(p j) -> p j", p=P))
-            if i == 2:
+            if i == BIAS_AT:
                 nc.sync.dma_start(out=bias_bc[:], in_=bias.partition_broadcast(P))
         premult(0)
         for i in range(n_pairs):
             if i + AHEAD < n_pairs:
                 load(i + AHEAD)
+            if i >= 2 and ORDER[i - 2][0] == "x" and ORDER[i - 2][1] in GRAM:
+                diagonal(i - 2, 0)
+                diagonal(i - 2, 1)
             for n in pending_dot:
-                ssq(0, n)
-            if i >= 1:
-                quantise(i - 1)
+                dot(0, n)
+            if i >= LAG:
+                quantise(i - LAG)
+            transpose_and_copy(i)
             if i + 1 < n_pairs:
                 premult(i + 1)
-            transpose_and_copy(i)
-            if i == 1:
-                bm = bias_map()
+            if i == XN_AT:
+                xn_batch1()
+            if i == XN_AT + 1:
+                xn_batch2()
             if i == 2:
+                bm = bias_map()
+            if i == 3:
                 bias_map2(*bm)
             for n in pending_mm:
                 mx_block(0, n)
+            if i >= 1 and ORDER[i - 1][0] == "x" and ORDER[i - 1][1] in GRAM:
+                gram(i - 1)
             for n in pending_dot:
-                dot(0, n)
+                ssq(0, n)
             pending_dot = pending_mm
             pending_mm = []
-            if i >= 1:
-                kind, c = ORDER[i - 1]
-                if kind == "w" and c % 2 == 1:
+            if i >= LAG:
+                kind, c = ORDER[i - LAG]
+                if kind == "w" and c % 2 == 1 and c // 2 < EARLY:
                     pending_mm = [c // 2]
-            if ORDER[i][0] == "x":
-                norms += [(i, 0, 0), (i, 0, 1), (i, 1, 0), (i, 1, 1)]
-            for j in range(2):
+            for j in range(NORM_RATE[i]):
                 if norms:
                     x_norm(*norms.pop(0))
-        for nm in norms:
-            x_norm(*nm)
-        xn_batch()
-        quantise(n_pairs - 1)
-        for n in pending_dot:
-            ssq(0, n)
-            dot(0, n)
         for n in pending_mm:
             mx_block(0, n)
-            ssq(0, n)
+        for n in pending_dot + pending_mm:
             dot(0, n)
-        mx_block(0, NB - 1)
-        ssq(0, NB - 1)
-        dot(0, NB - 1)
-        chain_a(0)
+            ssq(0, n)
+        for i in range(n_pairs - LAG, n_pairs - 1):
+            quantise(i)
+        for n in range(EARLY, NB):
+            mx_block(0, n)
+            ssq(0, n)
         new_sums(1)
+        for n in range(EARLY, NB):
+            dot(0, n)
+        quantise(n_pairs - 1)
+        chain_a(0)
         for n in range(NB):
             mx_block(1, n)
             ssq(1, n)
@@ -382,6 +436,9 @@ def tile_hypequalizedlinear_kernel(tc, x, weight, bias, out):
                     dot(r + 1, n)
             for n in range(NB):
                 zrow(r, n)
+                if r == NT - 1:
+                    leaky(r, n, 1)
+                    scale_store(r, n, 1)
                 if r + 1 < NT:
                     if n == 1:
                         chain_v1(r + 1)
@@ -399,9 +456,11 @@ def tile_hypequalizedlinear_kernel(tc, x, weight, bias, out):
                 chain_a(r + 2)
             if r + 1 < NT:
                 chain_c2(r + 1)
-            leaky(r, 0)
-            scale_store(r, 0)
+            if r == NT - 1:
+                break
+            leaky(r, 0, 2)
+            scale_store(r, 0, 2)
             if r + 2 < NT:
                 chain_t(r + 2)
-            leaky(r, 1)
-            scale_store(r, 1)
+            leaky(r, 2, 2)
+            scale_store(r, 2, 2)

@@ -21,15 +21,13 @@ NT = B // P
 NB = DOUT // 512
 
 ORDER = [(s[0], int(s[1])) for s in "w0 w1 x0 w2 w3 x1 w4 w5 x2 w6 w7 x3".split()]
-W_PAT = ["VVVP"] * 5 + ["VVPP"] * 3
-X_PAT = ["SSSS", "SSSS", "SSSS", "VSVV"]
-T_BANKS = [4, 5, 6, 7, 2, 3]
-EARLY = 2
-NORM_RATE = [0, 0, 0, 1, 1, 1, 1, 1, 1, 2, 0, 0]
+W_PAT = ["VVVP"] * 8
+X_PAT = ["VSSS", "VSVS", "VSVS", "VVVV"]
+T_BANKS = [4, 5, 6, 7]
+EARLY = 3
+NORM_RATE = [0, 0, 2, 2, 0, 2, 2, 2, 2, 2, 2, 0]
 LOADS = [(s[0], int(s[1])) for s in "w0 w1 x0 w2 w3 x1 w4 x3 w5 x2 w6 w7".split()]
-GRAM = (1, 2)
-XN_AT = 10
-LAG = 2
+LAG = 1
 BIAS_AT = 4
 AHEAD = 5
 
@@ -51,6 +49,8 @@ def tile_hypequalizedlinear_kernel(tc, x, weight, bias, out):
         psum = ctx.enter_context(tc.psum_pool(name="psum", bufs=1))
         ctx.enter_context(tc.manual_schedule())
 
+        dum = const.tile([P, 512], BF16, name="dum")
+        nc.vector.memset(dum[:], 0.0)
         ident = const.tile([P, P], F32, name="ident")
         make_identity(nc, ident[:])
         mh8 = const.tile([P, NT], F32, name="mh8")
@@ -70,7 +70,6 @@ def tile_hypequalizedlinear_kernel(tc, x, weight, bias, out):
         ws = const.tile([P, NG, DOUT], U8, name="ws", align_bytes=64)
         xn2 = const.tile([P, 2, NT], F32, name="xn2")
         q = const.tile([P, NT], F32, name="q")
-        nc.gpsimd.memset(xn2[:], 0.0)
         y2 = const.tile([P, 1], F32, name="y2")
         nscb = const.tile([P, 1], F32, name="nscb")
         ny4 = const.tile([P, 1], F32, name="ny4")
@@ -103,7 +102,13 @@ def tile_hypequalizedlinear_kernel(tc, x, weight, bias, out):
                         nc.vector.tensor_scalar(out=raw[ORDER[i]][:, :, sl], in0=raw[ORDER[i]][:, :, sl], scalar1=0.1,
                                                 scalar2=None, op0=ALU.mult)
 
-        def transpose_and_copy(i):
+        warm_ps = psum.tile([P, 512], F32, tag="bk3", name="warm_ps")
+
+        def warm_up(k):
+            for j in range(k):
+                nc.tensor.matmul(out=warm_ps[:], lhsT=dum[:, 0:P], rhs=dum[:], start=True, stop=True)
+
+        def transpose_and_copy(i, busy):
             kind, c = ORDER[i]
             words = raw[ORDER[i]][:].bitcast(F32)
             gt = gp.tile([P, NG, 256, 4], BF16, name="gt", align_bytes=64)
@@ -115,6 +120,8 @@ def tile_hypequalizedlinear_kernel(tc, x, weight, bias, out):
                     for a in range(2):
                         nc.tensor.transpose(tp[:, u, a, :], words[:, a, 256 * g + u:256 * g + 256:2],
                                             ident[:])
+                if g == 1 or (g == 3 and not busy):
+                    warm_up(2)
                 who = X_PAT[c][g] if kind == "x" else W_PAT[c][g]
                 fout = gt[:, g, :, :].rearrange("p j (u e) -> p j u e", e=2)
                 fin = tp[:].bitcast(BF16).rearrange("p u a (r e) -> p (a r) u e", e=2)
@@ -148,25 +155,6 @@ def tile_hypequalizedlinear_kernel(tc, x, weight, bias, out):
             jx = jkp.tile([P, 1024], BF16, name="jx", tag="jx")
             nc.scalar.activation(out=jx[:], in_=raw[("x", c)][:, a, 1024 * h:1024 * h + 1024], func=ACT.Square,
                                  accum_out=xn2[:, h, 2 * c + a:2 * c + a + 1])
-
-        gram_t = {}
-
-        def gram(i):
-            gt = grouped[i]
-            gr = psum.tile([P, 2, P], F32, tag="bk3", name="gr")
-            gram_t[i] = gr
-            for a in range(2):
-                for g in range(NG):
-                    for j in range(4):
-                        v = gt[:, g, 128 * a:128 * a + 128, j]
-                        nc.tensor.matmul(out=gr[:, a, :], lhsT=v, rhs=v, start=(g == 0 and j == 0),
-                                         stop=(g == NG - 1 and j == 3))
-
-        def diagonal(i, a):
-            r = 2 * ORDER[i][1] + a
-            jd = jkp.tile([P, P], F32, name="jd", tag="jd")
-            nc.vector.scalar_tensor_tensor(out=jd[:], in0=gram_t[i][:, a, :], scalar=1.0, in1=ident[:],
-                                           op0=ALU.mult, op1=ALU.mult, accum_out=xn2[:, 0, r:r + 1])
 
         banks = {}
 
@@ -352,7 +340,7 @@ def tile_hypequalizedlinear_kernel(tc, x, weight, bias, out):
             nc.sync.dma_start(out=out_v[r][:, sl], in_=z[:, sl])
 
         n_pairs = len(ORDER)
-        norms = [(c, a, h) for c in range(4) if c not in GRAM for a in range(2) for h in range(2)]
+        norms = [(c, a, h) for c in (0, 1, 3, 2) for a in range(2) for h in range(2)]
         new_sums(0)
         pending_mm = []
         pending_dot = []
@@ -363,31 +351,23 @@ def tile_hypequalizedlinear_kernel(tc, x, weight, bias, out):
             if i == BIAS_AT:
                 nc.sync.dma_start(out=bias_bc[:], in_=bias.partition_broadcast(P))
         premult(0)
+        warm_up(5)
         for i in range(n_pairs):
             if i + AHEAD < n_pairs:
                 load(i + AHEAD)
-            if i >= 2 and ORDER[i - 2][0] == "x" and ORDER[i - 2][1] in GRAM:
-                diagonal(i - 2, 0)
-                diagonal(i - 2, 1)
             for n in pending_dot:
                 dot(0, n)
             if i >= LAG:
                 quantise(i - LAG)
-            transpose_and_copy(i)
+            transpose_and_copy(i, pending_mm)
             if i + 1 < n_pairs:
                 premult(i + 1)
-            if i == XN_AT:
-                xn_batch1()
-            if i == XN_AT + 1:
-                xn_batch2()
             if i == 2:
                 bm = bias_map()
             if i == 3:
                 bias_map2(*bm)
             for n in pending_mm:
                 mx_block(0, n)
-            if i >= 1 and ORDER[i - 1][0] == "x" and ORDER[i - 1][1] in GRAM:
-                gram(i - 1)
             for n in pending_dot:
                 ssq(0, n)
             pending_dot = pending_mm
@@ -397,8 +377,9 @@ def tile_hypequalizedlinear_kernel(tc, x, weight, bias, out):
                 if kind == "w" and c % 2 == 1 and c // 2 < EARLY:
                     pending_mm = [c // 2]
             for j in range(NORM_RATE[i]):
-                if norms:
-                    x_norm(*norms.pop(0))
+                x_norm(*norms.pop(0))
+                if not norms:
+                    xn_batch1()
         for n in pending_mm:
             mx_block(0, n)
         for n in pending_dot + pending_mm:
@@ -412,6 +393,7 @@ def tile_hypequalizedlinear_kernel(tc, x, weight, bias, out):
         new_sums(1)
         for n in range(EARLY, NB):
             dot(0, n)
+        xn_batch2()
         quantise(n_pairs - 1)
         chain_a(0)
         for n in range(NB):

@@ -22,10 +22,10 @@ NB = DOUT // 512
 
 ORDER = [(s[0], int(s[1])) for s in "w0 w1 x0 w2 w3 x1 w4 w5 x2 w6 w7 x3".split()]
 W_PAT = ["VVVP"] * 8
-X_PAT = ["VSSS", "VSVS", "VSVS", "VVVV"]
-T_BANKS = [4, 5, 6, 7]
-EARLY = 3
-NORM_RATE = [0, 0, 2, 2, 0, 2, 2, 2, 2, 2, 2, 0]
+X_PAT = ["SSSV", "SSVV", "SSVV", "VSVV"]
+T_BANKS = [4, 5, 6, 7, 2, 3]
+EARLY = 2
+NORM_RATE = [0, 0, 2, 2, 0, 3, 2, 2, 3, 2, 0, 0]
 LOADS = [(s[0], int(s[1])) for s in "w0 w1 x0 w2 w3 x1 w4 x3 w5 x2 w6 w7".split()]
 LAG = 1
 BIAS_AT = 4
@@ -42,21 +42,17 @@ def tile_hypequalizedlinear_kernel(tc, x, weight, bias, out):
         const = ctx.enter_context(tc.tile_pool(name="const", bufs=1))
         xin = ctx.enter_context(tc.tile_pool(name="xin", bufs=4))
         win = ctx.enter_context(tc.tile_pool(name="win", bufs=5))
-        gp = ctx.enter_context(tc.tile_pool(name="gp", bufs=4))
+        gp = ctx.enter_context(tc.tile_pool(name="gp", bufs=3))
         zp = ctx.enter_context(tc.tile_pool(name="zp", bufs=3))
         jkp = ctx.enter_context(tc.tile_pool(name="jkp", bufs=2))
         sm = ctx.enter_context(tc.tile_pool(name="sm", bufs=4))
         psum = ctx.enter_context(tc.psum_pool(name="psum", bufs=1))
         ctx.enter_context(tc.manual_schedule())
 
-        dum = const.tile([P, 512], BF16, name="dum")
-        nc.vector.memset(dum[:], 0.0)
         ident = const.tile([P, P], F32, name="ident")
         make_identity(nc, ident[:])
         mh8 = const.tile([P, NT], F32, name="mh8")
         nc.gpsimd.memset(mh8[:], -0.5)
-        m1 = const.tile([P, 1], F32, name="m1")
-        nc.gpsimd.memset(m1[:], -1.0)
         tiny = const.tile([P, 1], F32, name="tiny")
         nc.gpsimd.memset(tiny[:], 2.0 ** -102)
         ones = const.tile([P, P], F32, name="ones")
@@ -102,13 +98,7 @@ def tile_hypequalizedlinear_kernel(tc, x, weight, bias, out):
                         nc.vector.tensor_scalar(out=raw[ORDER[i]][:, :, sl], in0=raw[ORDER[i]][:, :, sl], scalar1=0.1,
                                                 scalar2=None, op0=ALU.mult)
 
-        warm_ps = psum.tile([P, 512], F32, tag="bk3", name="warm_ps")
-
-        def warm_up(k):
-            for j in range(k):
-                nc.tensor.matmul(out=warm_ps[:], lhsT=dum[:, 0:P], rhs=dum[:], start=True, stop=True)
-
-        def transpose_and_copy(i, busy):
+        def transpose_and_copy(i):
             kind, c = ORDER[i]
             words = raw[ORDER[i]][:].bitcast(F32)
             gt = gp.tile([P, NG, 256, 4], BF16, name="gt", align_bytes=64)
@@ -120,8 +110,6 @@ def tile_hypequalizedlinear_kernel(tc, x, weight, bias, out):
                     for a in range(2):
                         nc.tensor.transpose(tp[:, u, a, :], words[:, a, 256 * g + u:256 * g + 256:2],
                                             ident[:])
-                if g == 1 or (g == 3 and not busy):
-                    warm_up(2)
                 who = X_PAT[c][g] if kind == "x" else W_PAT[c][g]
                 fout = gt[:, g, :, :].rearrange("p j (u e) -> p j u e", e=2)
                 fin = tp[:].bitcast(BF16).rearrange("p u a (r e) -> p (a r) u e", e=2)
@@ -173,31 +161,30 @@ def tile_hypequalizedlinear_kernel(tc, x, weight, bias, out):
 
         ge = nc.gpsimd
 
+        def col(nm, w=1):
+            return sm.tile([P, w], F32, name=nm, tag=nm)
+
         xnt = {}
 
         def xn_batch1():
-            xc2 = sm.tile([P, NT], F32, name="xc2", bufs=1)
-            ge.tensor_tensor(out=xc2[:], in0=xn2[:, 0, :], in1=xn2[:, 1, :], op=ALU.add)
-            ge.tensor_scalar(out=xc2[:], in0=xc2[:], scalar1=1e-30, scalar2=None, op0=ALU.max)
-            rxn = sm.tile([P, NT], F32, name="rxn", bufs=1)
-            ge.tensor_tensor(out=rxn[:], in0=xc2[:], in1=mh8[:], op=ALU.pow)
-            v = sm.tile([P, NT], F32, name="v", bufs=1)
-            ge.tensor_tensor(out=v[:], in0=xc2[:], in1=rxn[:], op=ALU.mult)
-            ge.tensor_scalar(out=v[:], in0=v[:], scalar1=1.0 - 1e-5, scalar2=None, op0=ALU.min)
-            xnt["v"], xnt["rxn"] = v, rxn
+            xnt["xc2"], xnt["rxn"] = col("xc2", NT), col("rxn", NT)
+            nc.vector.scalar_tensor_tensor(out=xnt["xc2"][:], in0=xn2[:, 0, :], scalar=1e-30, in1=xn2[:, 1, :],
+                                           op0=ALU.max, op1=ALU.add)
+            ge.tensor_tensor(out=xnt["rxn"][:], in0=xnt["xc2"][:], in1=mh8[:], op=ALU.pow)
 
         def xn_batch2():
-            v, rxn = xnt["v"], xnt["rxn"]
-            l1 = sm.tile([P, NT], F32, name="l1", bufs=1)
-            l2 = sm.tile([P, NT], F32, name="l2", bufs=1)
+            v, l1, l2, d = col("v8", NT), col("l1", NT), col("l2", NT), col("d8", NT)
+            nc.vector.tensor_tensor(out=v[:], in0=xnt["xc2"][:], in1=xnt["rxn"][:], op=ALU.mult)
+            nc.vector.tensor_scalar(out=v[:], in0=v[:], scalar1=1.0 - 1e-5, scalar2=None, op0=ALU.min)
             nc.scalar.activation(out=l1[:], in_=v[:], func=ACT.Ln, bias=1.0, scale=1.0)
             nc.scalar.activation(out=l2[:], in_=v[:], func=ACT.Ln, bias=1.0, scale=-1.0)
-            d = sm.tile([P, NT], F32, name="d", bufs=1)
-            ge.tensor_tensor(out=d[:], in0=l1[:], in1=l2[:], op=ALU.subtract)
-            ge.tensor_tensor(out=d[:], in0=d[:], in1=rxn[:], op=ALU.mult)
-            ge.tensor_scalar(out=q[:], in0=d[:], scalar1=0.5, scalar2=None, op0=ALU.mult)
-            warm = sm.tile([P, 1], F32, name="warm", bufs=1)
-            nc.scalar.activation(out=warm[:], in_=y2[:], func=ACT.Tanh)
+            xnt["d"], xnt["l"] = d, (l1, l2)
+
+        def xn_batch3():
+            (l1, l2), d = xnt["l"], xnt["d"]
+            nc.vector.tensor_tensor(out=d[:], in0=l1[:], in1=l2[:], op=ALU.subtract)
+            nc.vector.scalar_tensor_tensor(out=q[:], in0=d[:], scalar=0.5, in1=xnt["rxn"][:],
+                                           op0=ALU.mult, op1=ALU.mult)
 
         def bias_map():
             jb = sm.tile([P, DOUT // P], F32, name="jb", bufs=1)
@@ -214,21 +201,27 @@ def tile_hypequalizedlinear_kernel(tc, x, weight, bias, out):
             return u2, run
 
         def bias_map2(u2, run):
-            tb = sm.tile([P, 1], F32, name="tb", bufs=1)
-            nc.scalar.activation(out=tb[:], in_=u2[:], func=ACT.Tanh, scale=run[:, 0:1])
-            ge.tensor_scalar(out=nscb[:], in0=tb[:], scalar1=run[:, 0:1], scalar2=-0.1,
-                             op0=ALU.mult, op1=ALU.mult)
-            ge.tensor_tensor(out=y2[:], in0=tb[:], in1=tb[:], op=ALU.mult)
-            rnb = sm.tile([P, 1], F32, name="rnb", bufs=1)
-            nb2 = sm.tile([P, 1], F32, name="nb2", bufs=1)
-            ge.tensor_scalar(out=nb2[:], in0=nscb[:], scalar1=-1.0, scalar2=None, op0=ALU.mult)
-            ge.tensor_tensor(out=rnb[:], in0=nb2[:], in1=m1[:], op=ALU.pow)
-            y4 = sm.tile([P, 1], F32, name="y4", bufs=1)
-            ge.tensor_scalar(out=y4[:], in0=y2[:], scalar1=1.0, scalar2=-0.25, op0=ALU.add, op1=ALU.mult)
-            ge.tensor_tensor(out=ny4[:], in0=y4[:], in1=rnb[:], op=ALU.mult)
+            bmt["run"], bmt["tb"] = run, col("tb")
+            nc.scalar.activation(out=bmt["tb"][:], in_=u2[:], func=ACT.Tanh, scale=run[:, 0:1])
 
+        def bias_map3(i):
+            tb = bmt["tb"]
+            if i == 0:
+                nc.vector.tensor_scalar(out=nscb[:], in0=tb[:], scalar1=bmt["run"][:, 0:1], scalar2=-0.1,
+                                        op0=ALU.mult, op1=ALU.mult)
+                nc.vector.tensor_tensor(out=y2[:], in0=tb[:], in1=tb[:], op=ALU.mult)
+            elif i == 1:
+                bmt["rnb"], bmt["y4"] = col("rnb"), col("y4")
+                nc.vector.reciprocal(out=bmt["rnb"][:], in_=nscb[:])
+                nc.vector.tensor_scalar(out=bmt["y4"][:], in0=y2[:], scalar1=1.0, scalar2=0.25,
+                                        op0=ALU.add, op1=ALU.mult)
+            else:
+                nc.vector.tensor_tensor(out=ny4[:], in0=bmt["y4"][:], in1=bmt["rnb"][:], op=ALU.mult)
+
+        bmt = {}
         sums = {}
         coef = {}
+        pows = {}
         zt = {}
 
         def new_sums(r):
@@ -246,79 +239,87 @@ def tile_hypequalizedlinear_kernel(tc, x, weight, bias, out):
                                            op0=ALU.mult, op1=ALU.mult,
                                            accum_out=sums[r][1][:, n:n + 1])
 
-        def col(nm, w=1):
-            return sm.tile([P, w], F32, name=nm, tag=nm)
-
         def chain_a(r):
-            y, yq, rmn = col("y"), col("yq"), col("rmn")
-            coef[r] = {"yq": yq, "rmn": rmn}
+            k = coef.setdefault(r, {})
+            k["yq"] = col("yq")
+            pw = pows.setdefault(r, col("pw", 2))
             j4 = col("j4", NB)
             nc.scalar.activation(out=j4[:], in_=sums[r][0][:], func=ACT.Identity, bias=tiny[:, 0:1],
-                                 accum_out=y[:])
-            nc.scalar.activation(out=yq[:], in_=y[:], func=ACT.Copy, scale=q[:, r:r + 1])
-            ge.tensor_tensor(out=rmn[:], in0=y[:], in1=mh8[:, 0:1], op=ALU.pow)
+                                 accum_out=pw[:, 0:1])
+            nc.scalar.activation(out=k["yq"][:], in_=pw[:, 0:1], func=ACT.Copy, scale=q[:, r:r + 1])
+
+        def chain_p(r):
+            rt = col("rt", 2)
+            if r in (0, NT):
+                lo, hi = (0, 1) if r == 0 else (1, 2)
+                ge.tensor_tensor(out=rt[:, lo:hi], in0=pows[r][:, lo:hi], in1=mh8[:, 0:1], op=ALU.pow)
+            else:
+                ge.tensor_tensor(out=rt[:], in0=pows[r][:], in1=mh8[:, 0:2], op=ALU.pow)
+            if r < NT:
+                coef[r]["rmn"] = rt[:, 0:1]
+            if r > 0:
+                coef[r - 1]["pr"] = rt[:, 1:2]
 
         def chain_t(r):
             k = coef[r]
-            th, x2 = col("th"), col("x2")
-            k["th"], k["x2"] = th, x2
-            nc.scalar.activation(out=th[:], in_=k["yq"][:], func=ACT.Tanh, scale=k["rmn"][:, 0:1])
-            nc.scalar.activation(out=x2[:], in_=th[:], func=ACT.Square)
-
-        def chain_v1(r):
-            k = coef[r]
-            k["nbc"] = col("nbc")
-            nc.vector.tensor_scalar(out=k["nbc"][:], in0=k["x2"][:], scalar1=1.0, scalar2=-1e-18,
-                                    op0=ALU.subtract, op1=ALU.min)
-
-        def chain_v2(r):
-            k = coef[r]
-            k["rn"] = col("rn")
-            nc.vector.reciprocal(out=k["rn"][:], in_=k["nbc"][:])
+            k["th"], k["s"] = col("th"), col("s")
+            nc.scalar.activation(out=k["th"][:], in_=k["yq"][:], func=ACT.Tanh, scale=k["rmn"])
 
         def chain_s(r):
             k = coef[r]
-            s, w, sw, yw = col("s"), col("w"), col("sw"), col("yw")
-            k["s"], k["sw"], k["yw"] = s, sw, yw
-            nc.scalar.activation(out=s[:], in_=k["th"][:], func=ACT.Copy, scale=k["rmn"][:, 0:1])
-            nc.scalar.activation(out=w[:], in_=s[:], func=ACT.Copy, scale=k["rn"][:, 0:1])
-            nc.scalar.activation(out=sw[:], in_=s[:], func=ACT.Copy, scale=w[:, 0:1])
-            nc.scalar.activation(out=yw[:], in_=w[:], func=ACT.Copy, scale=ny4[:, 0:1])
+            nc.scalar.activation(out=k["s"][:], in_=k["th"][:], func=ACT.Copy, scale=k["rmn"])
+
+        def chain_v(r, i):
+            k = coef[r]
+            if i == 0:
+                k["a1"] = col("a1")
+                nc.vector.tensor_scalar(out=k["a1"][:], in0=k["th"][:], scalar1=k["th"][:, 0:1], scalar2=1.0,
+                                        op0=ALU.mult, op1=ALU.subtract)
+            elif i == 1:
+                k["nbc"] = col("nbc")
+                nc.vector.tensor_scalar(out=k["nbc"][:], in0=k["a1"][:], scalar1=-1e-18, scalar2=None,
+                                        op0=ALU.min)
+            else:
+                k["rn"] = col("rn")
+                nc.vector.reciprocal(out=k["rn"][:], in_=k["nbc"][:])
+
+        def chain_d(r):
+            k = coef[r]
+            k["t1"], k["ts"], k["xa"] = col("t1"), col("ts"), col("xa")
+            j4 = col("j4", NB)
+            nc.scalar.activation(out=j4[:], in_=sums[r][1][:], func=ACT.Identity, scale=k["s"][:, 0:1],
+                                 bias=ny4[:, 0:1], accum_out=k["t1"][:])
+            nc.scalar.activation(out=k["ts"][:], in_=k["t1"][:], func=ACT.Copy, scale=k["s"][:, 0:1])
+            nc.scalar.activation(out=k["xa"][:], in_=k["t1"][:], func=ACT.Copy, scale=nscb[:, 0:1])
 
         def chain_g(r):
             k = coef[r]
-            ga = col("ga")
-            k["ga"] = ga
-            j4 = col("j4", NB)
-            nc.scalar.activation(out=j4[:], in_=sums[r][1][:], func=ACT.Identity, scale=k["sw"][:, 0:1],
-                                 bias=k["yw"][:, 0:1], accum_out=ga[:])
+            k["ga"] = col("ga")
+            nc.scalar.activation(out=k["ga"][:], in_=k["ts"][:], func=ACT.Copy, scale=k["rn"][:, 0:1])
 
-        def chain_c1(r):
+        def chain_n(r):
             k = coef[r]
-            xs, nb, hd, xy, dn = col("xs"), col("nb", 2), col("hd", 2), col("xy"), col("dn", 2)
-            k["dn"] = dn
-            dt = sums[r][1]
-            ge.tensor_tensor(out=hd[:], in0=dt[:, 0:2], in1=dt[:, 2:4], op=ALU.add)
-            ge.tensor_tensor(out=xs[:], in0=k["s"][:], in1=nscb[:], op=ALU.mult)
-            ge.tensor_scalar(out=nb[:, 0:1], in0=k["x2"][:], scalar1=y2[:, 0:1], scalar2=1.0,
-                             op0=ALU.mult, op1=ALU.add)
-            ge.tensor_scalar(out=nb[:, 1:2], in0=k["x2"][:], scalar1=y2[:, 0:1], scalar2=None, op0=ALU.add)
-            ge.tensor_scalar(out=xy[:], in0=hd[:, 0:1], scalar1=hd[:, 1:2], scalar2=xs[:, 0:1],
-                             op0=ALU.add, op1=ALU.mult)
-            ge.tensor_scalar(out=dn[:], in0=nb[:], scalar1=xy[:, 0:1], scalar2=None, op0=ALU.add)
+            k["dn0"], k["dn1"], k["bcs"] = col("dn0"), col("dn1"), col("bcs")
+            nc.scalar.activation(out=k["dn0"][:], in_=k["nbc"][:], func=ACT.Identity, scale=y2[:, 0:1],
+                                 bias=k["xa"][:, 0:1])
+            nc.scalar.activation(out=k["dn1"][:], in_=k["nbc"][:], func=ACT.Identity, bias=k["xa"][:, 0:1])
+            nc.scalar.activation(out=k["bcs"][:], in_=k["nbc"][:], func=ACT.Copy, scale=nscb[:, 0:1])
 
-        def chain_c2(r):
+        def chain_m(r, i):
             k = coef[r]
-            mx, pd, pr, be = col("mx"), col("pd"), col("pr"), col("be")
-            k["be"] = be
-            dn = k["dn"]
-            ge.tensor_scalar(out=mx[:], in0=dn[:, 1:2], scalar1=1.0 / (0.999 * 0.999),
-                             scalar2=dn[:, 0:1], op0=ALU.mult, op1=ALU.max)
-            ge.tensor_scalar(out=pd[:], in0=mx[:], scalar1=dn[:, 0:1], scalar2=1e-30,
-                             op0=ALU.mult, op1=ALU.max)
-            ge.tensor_tensor(out=pr[:], in0=pd[:], in1=mh8[:, 0:1], op=ALU.pow)
-            ge.tensor_scalar(out=be[:], in0=pr[:], scalar1=k["nbc"][:, 0:1], scalar2=nscb[:, 0:1],
-                             op0=ALU.mult, op1=ALU.mult)
+            if i == 0:
+                k["mx"] = col("mx")
+                nc.vector.tensor_scalar(out=k["mx"][:], in0=k["dn1"][:], scalar1=1.0 / (0.999 * 0.999),
+                                        scalar2=k["dn0"][:, 0:1], op0=ALU.mult, op1=ALU.max)
+            else:
+                pw = pows.setdefault(r + 1, col("pw", 2))
+                nc.vector.tensor_scalar(out=pw[:, 1:2], in0=k["mx"][:], scalar1=k["dn0"][:, 0:1],
+                                        scalar2=1e-30, op0=ALU.mult, op1=ALU.max)
+
+        def chain_b(r):
+            k = coef[r]
+            k["be"] = col("be")
+            nc.scalar.activation(out=k["be"][:], in_=k["pr"], func=ACT.Copy, scale=k["bcs"][:, 0:1])
 
         def zrow(r, n):
             if n == 0:
@@ -350,8 +351,9 @@ def tile_hypequalizedlinear_kernel(tc, x, weight, bias, out):
                 nc.sync.dma_start(out=bias_p[:], in_=bias.rearrange("(p j) -> p j", p=P))
             if i == BIAS_AT:
                 nc.sync.dma_start(out=bias_bc[:], in_=bias.partition_broadcast(P))
+        warm = sm.tile([P, 1], F32, name="warm", bufs=1)
+        nc.scalar.activation(out=warm[:], in_=ones[:, 0:1], func=ACT.Ln)
         premult(0)
-        warm_up(5)
         for i in range(n_pairs):
             if i + AHEAD < n_pairs:
                 load(i + AHEAD)
@@ -359,13 +361,13 @@ def tile_hypequalizedlinear_kernel(tc, x, weight, bias, out):
                 dot(0, n)
             if i >= LAG:
                 quantise(i - LAG)
-            transpose_and_copy(i, pending_mm)
+            if i == n_pairs - 1:
+                xn_batch2()
+            transpose_and_copy(i)
             if i + 1 < n_pairs:
                 premult(i + 1)
             if i == 2:
                 bm = bias_map()
-            if i == 3:
-                bias_map2(*bm)
             for n in pending_mm:
                 mx_block(0, n)
             for n in pending_dot:
@@ -378,8 +380,11 @@ def tile_hypequalizedlinear_kernel(tc, x, weight, bias, out):
                     pending_mm = [c // 2]
             for j in range(NORM_RATE[i]):
                 x_norm(*norms.pop(0))
-                if not norms:
-                    xn_batch1()
+            if i == n_pairs - 2:
+                xn_batch1()
+            if i == n_pairs - 1:
+                bias_map2(*bm)
+                xn_batch3()
         for n in pending_mm:
             mx_block(0, n)
         for n in pending_dot + pending_mm:
@@ -391,58 +396,106 @@ def tile_hypequalizedlinear_kernel(tc, x, weight, bias, out):
             mx_block(0, n)
             ssq(0, n)
         new_sums(1)
-        for n in range(EARLY, NB):
-            dot(0, n)
-        xn_batch2()
+        bias_map3(0)
         quantise(n_pairs - 1)
+        bias_map3(1)
+        dot(0, EARLY)
+        bias_map3(2)
+        for n in range(EARLY + 1, NB):
+            dot(0, n)
         chain_a(0)
+        chain_p(0)
         for n in range(NB):
             mx_block(1, n)
-            ssq(1, n)
-            if n == 1:
-                chain_t(0)
-                chain_v1(0)
-            dot(1, n)
-            if n == 1:
-                chain_v2(0)
-                chain_s(0)
-                chain_g(0)
-                chain_c1(0)
+        dot(1, 0)
+        ssq(1, 0)
+        chain_t(0)
+        chain_s(0)
+        dot(1, 1)
+        chain_v(0, 0)
+        ssq(1, 1)
+        chain_d(0)
+        dot(1, 2)
+        chain_v(0, 1)
+        ssq(1, 2)
+        dot(1, 3)
+        chain_v(0, 2)
+        chain_g(0)
+        chain_n(0)
+        ssq(1, 3)
         chain_a(1)
-        chain_c2(0)
+        zrow(0, 0)
+        chain_m(0, 0)
+        zrow(0, 1)
+        chain_m(0, 1)
+        chain_p(1)
+        zrow(0, 2)
+        zrow(0, 3)
+        new_sums(2)
+        for n in range(NB):
+            mx_block(2, n)
         chain_t(1)
+        chain_s(1)
+        chain_d(1)
+        chain_b(0)
+        ssq(2, 0)
+        ssq(2, 1)
+        leaky(0, 0, 2)
+        chain_v(1, 0)
+        dot(2, 0)
+        chain_v(1, 1)
+        dot(2, 1)
+        chain_v(1, 2)
+        chain_g(1)
+        chain_n(1)
+        ssq(2, 2)
+        leaky(0, 2, 2)
+        ssq(2, 3)
+        dot(2, 2)
+        chain_m(1, 0)
+        dot(2, 3)
 
-        for r in range(NT):
-            if 1 <= r < NT - 1:
-                for n in range(NB):
-                    dot(r + 1, n)
+        for r in range(1, NT):
+            last = r == NT - 1
+            if not last:
+                chain_a(r + 1)
+            if 1 < r and not last:
+                dot(r + 1, 0)
+            chain_m(r, 1)
+            chain_p(r + 1)
+            if 1 < r and not last:
+                dot(r + 1, 1)
+            scale_store(r - 1, 0, 2)
+            if not last:
+                chain_t(r + 1)
+            chain_b(r)
+            scale_store(r - 1, 2, 2)
+            if not last:
+                chain_s(r + 1)
+                if 1 < r:
+                    dot(r + 1, 2)
+                    dot(r + 1, 3)
+                chain_d(r + 1)
             for n in range(NB):
                 zrow(r, n)
-                if r == NT - 1:
+                if not last and n < 3:
+                    chain_v(r + 1, n)
+                if last:
                     leaky(r, n, 1)
                     scale_store(r, n, 1)
-                if r + 1 < NT:
-                    if n == 1:
-                        chain_v1(r + 1)
-                    if n == 2:
-                        chain_v2(r + 1)
-            if r + 1 < NT:
-                chain_s(r + 1)
-                chain_g(r + 1)
-                chain_c1(r + 1)
+            if last:
+                break
             if r + 2 < NT:
                 new_sums(r + 2)
                 for n in range(NB):
                     mx_block(r + 2, n)
-                    ssq(r + 2, n)
-                chain_a(r + 2)
-            if r + 1 < NT:
-                chain_c2(r + 1)
-            if r == NT - 1:
-                break
-            leaky(r, 0, 2)
-            scale_store(r, 0, 2)
+                ssq(r + 2, 0)
+                ssq(r + 2, 1)
+            chain_g(r + 1)
+            chain_n(r + 1)
             if r + 2 < NT:
-                chain_t(r + 2)
+                ssq(r + 2, 2)
+                ssq(r + 2, 3)
+            leaky(r, 0, 2)
             leaky(r, 2, 2)
-            scale_store(r, 2, 2)
+            chain_m(r + 1, 0)

@@ -21,11 +21,11 @@ NT = B // P
 NB = DOUT // 512
 
 ORDER = [(s[0], int(s[1])) for s in "w0 w1 x0 w2 w3 x1 w4 w5 x2 w6 w7 x3".split()]
-W_PAT = ["VVVP"] * 8
-X_PAT = ["SSSV", "SSVV", "SSVV", "VSVV"]
-T_BANKS = [4, 5, 6, 7, 2, 3]
-EARLY = 2
-NORM_RATE = [0, 0, 2, 2, 0, 3, 2, 2, 3, 2, 0, 0]
+W_PAT = ["VSVS"] * 4 + ["VSVV"] * 4
+X_PAT = ["SSSS", "SSSS", "SSSS", "VSVV"]
+T_BANKS = [4, 5, 6, 7, 3]
+EARLY = 3
+NORM_RATE = [0, 0, 2, 2, 0, 2, 2, 2, 3, 3, 0, 0]
 LOADS = [(s[0], int(s[1])) for s in "w0 w1 x0 w2 w3 x1 w4 x3 w5 x2 w6 w7".split()]
 LAG = 1
 BIAS_AT = 4
@@ -42,6 +42,7 @@ def tile_hypequalizedlinear_kernel(tc, x, weight, bias, out):
         const = ctx.enter_context(tc.tile_pool(name="const", bufs=1))
         xin = ctx.enter_context(tc.tile_pool(name="xin", bufs=4))
         win = ctx.enter_context(tc.tile_pool(name="win", bufs=5))
+        wsp = ctx.enter_context(tc.tile_pool(name="wsp", bufs=3))
         gp = ctx.enter_context(tc.tile_pool(name="gp", bufs=3))
         zp = ctx.enter_context(tc.tile_pool(name="zp", bufs=3))
         jkp = ctx.enter_context(tc.tile_pool(name="jkp", bufs=2))
@@ -89,18 +90,30 @@ def tile_hypequalizedlinear_kernel(tc, x, weight, bias, out):
 
         turn = {"n": 0}
 
+        scaled = {}
+
         def premult(i):
+            if ORDER[i][0] == "x":
+                return
             kind, c = ORDER[i]
-            if kind == "w":
-                for g in range(NG):
-                    if W_PAT[c][g] == "P":
-                        sl = slice(512 * g, 512 * g + 512)
-                        nc.vector.tensor_scalar(out=raw[ORDER[i]][:, :, sl], in0=raw[ORDER[i]][:, :, sl], scalar1=0.1,
-                                                scalar2=None, op0=ALU.mult)
+            sp = wsp.tile([P, 2, NG, 2, P, 2], BF16, name="sp", align_bytes=64)
+            scaled[i] = sp
+            src = raw[ORDER[i]][:].rearrange("q a (g p u e) -> q a g u p e", g=NG, u=2, e=2)
+            if i == 0:
+                parts = [(sp[:, a, 2 * h:2 * h + 2, u, :, :], src[:, a, 2 * h:2 * h + 2, u, :, :])
+                         for h in range(2) for u in range(2) for a in range(2)]
+            else:
+                parts = [(sp[:].rearrange("q a g u p e -> q (a g) u p e")[:, :, u, :, :],
+                          src.rearrange("q a g u p e -> q (a g) u p e")[:, :, u, :, :]) for u in range(2)]
+            for dst, s in parts:
+                nc.vector.tensor_scalar(out=dst, in0=s, scalar1=0.1, scalar2=None, op0=ALU.mult)
 
         def transpose_and_copy(i):
             kind, c = ORDER[i]
-            words = raw[ORDER[i]][:].bitcast(F32)
+            if i in scaled:
+                words = scaled[i][:].rearrange("q a g u p e -> q a (g u p e)").bitcast(F32)
+            else:
+                words = raw[ORDER[i]][:].bitcast(F32)
             gt = gp.tile([P, NG, 256, 4], BF16, name="gt", align_bytes=64)
             grouped[i] = gt
             for g in range(NG):
@@ -108,18 +121,13 @@ def tile_hypequalizedlinear_kernel(tc, x, weight, bias, out):
                 turn["n"] += 1
                 for u in range(2):
                     for a in range(2):
-                        nc.tensor.transpose(tp[:, u, a, :], words[:, a, 256 * g + u:256 * g + 256:2],
-                                            ident[:])
+                        lo = 256 * g
+                        cols = slice(lo + 128 * u, lo + 128 * u + 128) if i in scaled else slice(lo + u, lo + 256, 2)
+                        nc.tensor.transpose(tp[:, u, a, :], words[:, a, cols], ident[:])
                 who = X_PAT[c][g] if kind == "x" else W_PAT[c][g]
-                fout = gt[:, g, :, :].rearrange("p j (u e) -> p j u e", e=2)
-                fin = tp[:].bitcast(BF16).rearrange("p u a (r e) -> p (a r) u e", e=2)
                 wout = gt[:, g, :, :].bitcast(F32)
                 win_ = tp[:].rearrange("p u a r -> p (a r) u")
-                if kind == "w" and who == "V":
-                    nc.vector.tensor_scalar(out=fout, in0=fin, scalar1=0.1, scalar2=None, op0=ALU.mult)
-                elif kind == "w" and who == "S":
-                    nc.scalar.activation(out=fout, in_=fin, func=ACT.Copy, scale=0.1)
-                elif who == "V":
+                if who == "V":
                     nc.vector.tensor_copy(out=wout, in_=win_)
                 else:
                     nc.scalar.copy(out=wout, in_=win_)

@@ -20,15 +20,17 @@ NG = DIN // 512
 NT = B // P
 NB = DOUT // 512
 
-ORDER = [(s[0], int(s[1])) for s in "w0 w1 x0 w2 w3 x1 w4 w5 x2 w6 w7 x3".split()]
-W_PAT = ["VSVS"] * 4 + ["VSVV"] * 4
-X_PAT = ["SSSS", "SSSS", "SSSS", "VSVV"]
+ORDER = [(s[0], int(s[1])) for s in "w0 x0 w1 w2 x1 w3 w4 x2 w5 w6 w7 x3".split()]
+W_PAT = ["FSFF"] * 8
+X_PAT = ["SSSS", "VSVS", "VSVS", "VVVV"]
 T_BANKS = [4, 5, 6, 7, 3]
 EARLY = 3
-NORM_RATE = [0, 0, 2, 2, 0, 2, 2, 2, 3, 3, 0, 0]
-LOADS = [(s[0], int(s[1])) for s in "w0 w1 x0 w2 w3 x1 w4 x3 w5 x2 w6 w7".split()]
+NORM_RATE = [0, 0, 2, 2, 2, 2, 2, 3, 3, 0, 0, 0]
+LOADS = [(s[0], int(s[1])) for s in "w0 x0 w1 x1 w2 x2 w3 x3 w4 w5 w6 w7".split()]
 LAG = 1
 BIAS_AT = 4
+XN = (9, 10, 11)
+NORM_ORDER = (0, 1, 2, 3)
 AHEAD = 5
 
 
@@ -59,6 +61,7 @@ def tile_hypequalizedlinear_kernel(tc, x, weight, bias, out):
         ones = const.tile([P, P], F32, name="ones")
         nc.gpsimd.memset(ones[:], 1.0)
 
+        bias_l = const.tile([P, 512], F32, name="bias_l")
         bias_bc = const.tile([P, DOUT], BF16, name="bias_bc")
         bias_p = const.tile([P, DOUT // P], BF16, name="bias_p")
         xc = const.tile([P, 4, NG, 256], U32, name="xc", align_bytes=64)
@@ -96,38 +99,50 @@ def tile_hypequalizedlinear_kernel(tc, x, weight, bias, out):
             if ORDER[i][0] == "x":
                 return
             kind, c = ORDER[i]
+            dry = [g for g in range(NG) if W_PAT[c][g] != "F"]
+            if not dry:
+                return
             sp = wsp.tile([P, 2, NG, 2, P, 2], BF16, name="sp", align_bytes=64)
             scaled[i] = sp
             src = raw[ORDER[i]][:].rearrange("q a (g p u e) -> q a g u p e", g=NG, u=2, e=2)
-            if i == 0:
-                parts = [(sp[:, a, 2 * h:2 * h + 2, u, :, :], src[:, a, 2 * h:2 * h + 2, u, :, :])
-                         for h in range(2) for u in range(2) for a in range(2)]
-            else:
+            if len(dry) == NG and i > 0:
                 parts = [(sp[:].rearrange("q a g u p e -> q (a g) u p e")[:, :, u, :, :],
                           src.rearrange("q a g u p e -> q (a g) u p e")[:, :, u, :, :]) for u in range(2)]
+            else:
+                step = dry[1] - dry[0] if len(dry) > 1 else 1
+                runs = [dry] if i > 0 and all(y - x == step for x, y in zip(dry, dry[1:])) else [[g] for g in dry]
+                parts = [(sp[:, a, r[0]:r[-1] + 1:step, u, :, :], src[:, a, r[0]:r[-1] + 1:step, u, :, :])
+                         for r in runs for u in range(2) for a in range(2)]
             for dst, s in parts:
                 nc.vector.tensor_scalar(out=dst, in0=s, scalar1=0.1, scalar2=None, op0=ALU.mult)
 
         def transpose_and_copy(i):
             kind, c = ORDER[i]
+            words = raw[ORDER[i]][:].bitcast(F32)
             if i in scaled:
-                words = scaled[i][:].rearrange("q a g u p e -> q a (g u p e)").bitcast(F32)
-            else:
-                words = raw[ORDER[i]][:].bitcast(F32)
+                packed = scaled[i][:].rearrange("q a g u p e -> q a (g u p e)").bitcast(F32)
             gt = gp.tile([P, NG, 256, 4], BF16, name="gt", align_bytes=64)
             grouped[i] = gt
             for g in range(NG):
                 tp = psum.tile([P, 2, 2, P], F32, tag="bk%d" % T_BANKS[turn["n"] % len(T_BANKS)], name="tp")
                 turn["n"] += 1
+                who = X_PAT[c][g] if kind == "x" else W_PAT[c][g]
+                lo = 256 * g
                 for u in range(2):
                     for a in range(2):
-                        lo = 256 * g
-                        cols = slice(lo + 128 * u, lo + 128 * u + 128) if i in scaled else slice(lo + u, lo + 256, 2)
-                        nc.tensor.transpose(tp[:, u, a, :], words[:, a, cols], ident[:])
-                who = X_PAT[c][g] if kind == "x" else W_PAT[c][g]
+                        if kind == "w" and who != "F":
+                            src = packed[:, a, lo + 128 * u:lo + 128 * u + 128]
+                        else:
+                            src = words[:, a, lo + u:lo + 256:2]
+                        nc.tensor.transpose(tp[:, u, a, :], src, ident[:])
                 wout = gt[:, g, :, :].bitcast(F32)
                 win_ = tp[:].rearrange("p u a r -> p (a r) u")
-                if who == "V":
+                if who == "F":
+                    nc.vector.tensor_scalar(
+                        out=gt[:, g, :, :].rearrange("p j (u e) -> p j u e", e=2),
+                        in0=tp[:].bitcast(BF16).rearrange("p u a (r e) -> p (a r) u e", e=2),
+                        scalar1=0.1, scalar2=None, op0=ALU.mult)
+                elif who == "V":
                     nc.vector.tensor_copy(out=wout, in_=win_)
                 else:
                     nc.scalar.copy(out=wout, in_=win_)
@@ -229,7 +244,6 @@ def tile_hypequalizedlinear_kernel(tc, x, weight, bias, out):
         bmt = {}
         sums = {}
         coef = {}
-        pows = {}
         zt = {}
 
         def new_sums(r):
@@ -249,33 +263,21 @@ def tile_hypequalizedlinear_kernel(tc, x, weight, bias, out):
 
         def chain_a(r):
             k = coef.setdefault(r, {})
-            k["yq"] = col("yq")
-            pw = pows.setdefault(r, col("pw", 2))
+            k["y"], k["yq"], k["rmn"] = col("y"), col("yq"), col("rmn")
             j4 = col("j4", NB)
             nc.scalar.activation(out=j4[:], in_=sums[r][0][:], func=ACT.Identity, bias=tiny[:, 0:1],
-                                 accum_out=pw[:, 0:1])
-            nc.scalar.activation(out=k["yq"][:], in_=pw[:, 0:1], func=ACT.Copy, scale=q[:, r:r + 1])
-
-        def chain_p(r):
-            rt = col("rt", 2)
-            if r in (0, NT):
-                lo, hi = (0, 1) if r == 0 else (1, 2)
-                ge.tensor_tensor(out=rt[:, lo:hi], in0=pows[r][:, lo:hi], in1=mh8[:, 0:1], op=ALU.pow)
-            else:
-                ge.tensor_tensor(out=rt[:], in0=pows[r][:], in1=mh8[:, 0:2], op=ALU.pow)
-            if r < NT:
-                coef[r]["rmn"] = rt[:, 0:1]
-            if r > 0:
-                coef[r - 1]["pr"] = rt[:, 1:2]
+                                 accum_out=k["y"][:])
+            nc.scalar.activation(out=k["yq"][:], in_=k["y"][:], func=ACT.Copy, scale=q[:, r:r + 1])
+            ge.tensor_tensor(out=k["rmn"][:], in0=k["y"][:], in1=mh8[:, 0:1], op=ALU.pow)
 
         def chain_t(r):
             k = coef[r]
             k["th"], k["s"] = col("th"), col("s")
-            nc.scalar.activation(out=k["th"][:], in_=k["yq"][:], func=ACT.Tanh, scale=k["rmn"])
+            nc.scalar.activation(out=k["th"][:], in_=k["yq"][:], func=ACT.Tanh, scale=k["rmn"][:, 0:1])
 
         def chain_s(r):
             k = coef[r]
-            nc.scalar.activation(out=k["s"][:], in_=k["th"][:], func=ACT.Copy, scale=k["rmn"])
+            nc.scalar.activation(out=k["s"][:], in_=k["th"][:], func=ACT.Copy, scale=k["rmn"][:, 0:1])
 
         def chain_v(r, i):
             k = coef[r]
@@ -320,21 +322,30 @@ def tile_hypequalizedlinear_kernel(tc, x, weight, bias, out):
                 nc.vector.tensor_scalar(out=k["mx"][:], in0=k["dn1"][:], scalar1=1.0 / (0.999 * 0.999),
                                         scalar2=k["dn0"][:, 0:1], op0=ALU.mult, op1=ALU.max)
             else:
-                pw = pows.setdefault(r + 1, col("pw", 2))
-                nc.vector.tensor_scalar(out=pw[:, 1:2], in0=k["mx"][:], scalar1=k["dn0"][:, 0:1],
+                k["pd"], k["pr"] = col("pd"), col("pr")
+                nc.vector.tensor_scalar(out=k["pd"][:], in0=k["mx"][:], scalar1=k["dn0"][:, 0:1],
                                         scalar2=1e-30, op0=ALU.mult, op1=ALU.max)
+                ge.tensor_tensor(out=k["pr"][:], in0=k["pd"][:], in1=mh8[:, 0:1], op=ALU.pow)
 
         def chain_b(r):
             k = coef[r]
             k["be"] = col("be")
-            nc.scalar.activation(out=k["be"][:], in_=k["pr"], func=ACT.Copy, scale=k["bcs"][:, 0:1])
+            nc.scalar.activation(out=k["be"][:], in_=k["pr"][:], func=ACT.Copy, scale=k["bcs"][:, 0:1])
 
         def zrow(r, n):
-            if n == 0:
+            if r not in zt:
                 zt[r] = zp.tile([P, DOUT], F32, name="z", tag="z")
             sl = slice(512 * n, 512 * n + 512)
             nc.vector.scalar_tensor_tensor(out=zt[r][:, sl], in0=banks[(r, n)][:], scalar=coef[r]["ga"][:, 0:1],
                                            in1=bias_bc[:, sl], op0=ALU.mult, op1=ALU.add)
+
+        def shifted(r):
+            if r not in zt:
+                zt[r] = zp.tile([P, DOUT], F32, name="z", tag="z")
+            sl = slice(1536, 2048)
+            nc.scalar.activation(out=zt[r][:, sl], in_=banks[(r, 3)][:], func=ACT.Copy,
+                                 scale=coef[r]["ga"][:, 0:1])
+            ge.tensor_tensor(out=zt[r][:, sl], in0=zt[r][:, sl], in1=bias_l[:], op=ALU.add)
 
         def leaky(r, n, k):
             sl = slice(512 * n, 512 * (n + k))
@@ -349,7 +360,7 @@ def tile_hypequalizedlinear_kernel(tc, x, weight, bias, out):
             nc.sync.dma_start(out=out_v[r][:, sl], in_=z[:, sl])
 
         n_pairs = len(ORDER)
-        norms = [(c, a, h) for c in (0, 1, 3, 2) for a in range(2) for h in range(2)]
+        norms = [(c, a, h) for c in NORM_ORDER for a in range(2) for h in range(2)]
         new_sums(0)
         pending_mm = []
         pending_dot = []
@@ -369,11 +380,11 @@ def tile_hypequalizedlinear_kernel(tc, x, weight, bias, out):
                 dot(0, n)
             if i >= LAG:
                 quantise(i - LAG)
-            if i == n_pairs - 1:
-                xn_batch2()
             transpose_and_copy(i)
             if i + 1 < n_pairs:
                 premult(i + 1)
+            if i == 6:
+                nc.scalar.copy(out=bias_l[:], in_=bias_bc[:, 1536:2048])
             if i == 2:
                 bm = bias_map()
             for n in pending_mm:
@@ -387,12 +398,16 @@ def tile_hypequalizedlinear_kernel(tc, x, weight, bias, out):
                 if kind == "w" and c % 2 == 1 and c // 2 < EARLY:
                     pending_mm = [c // 2]
             for j in range(NORM_RATE[i]):
-                x_norm(*norms.pop(0))
-            if i == n_pairs - 2:
+                if norms:
+                    x_norm(*norms.pop(0))
+            if i == XN[0]:
                 xn_batch1()
-            if i == n_pairs - 1:
+            if i == XN[1]:
+                xn_batch2()
+            if i == XN[2]:
                 bias_map2(*bm)
                 xn_batch3()
+        ROT = (3, 0, 1, 2)
         for n in pending_mm:
             mx_block(0, n)
         for n in pending_dot + pending_mm:
@@ -405,105 +420,106 @@ def tile_hypequalizedlinear_kernel(tc, x, weight, bias, out):
             ssq(0, n)
         new_sums(1)
         bias_map3(0)
-        quantise(n_pairs - 1)
-        bias_map3(1)
-        dot(0, EARLY)
-        bias_map3(2)
-        for n in range(EARLY + 1, NB):
+        for n in range(EARLY, NB):
             dot(0, n)
+        bias_map3(1)
         chain_a(0)
-        chain_p(0)
         for n in range(NB):
             mx_block(1, n)
         dot(1, 0)
-        ssq(1, 0)
+        bias_map3(2)
+        dot(1, 1)
         chain_t(0)
         chain_s(0)
-        dot(1, 1)
+        ssq(1, 0)
         chain_v(0, 0)
-        ssq(1, 1)
-        chain_d(0)
-        dot(1, 2)
+        quantise(n_pairs - 1)
         chain_v(0, 1)
-        ssq(1, 2)
-        dot(1, 3)
+        chain_d(0)
+        ssq(1, 1)
+        dot(1, 2)
         chain_v(0, 2)
         chain_g(0)
+        shifted(0)
+        ssq(1, 2)
         chain_n(0)
+        dot(1, 3)
         ssq(1, 3)
         chain_a(1)
-        zrow(0, 0)
-        chain_m(0, 0)
-        zrow(0, 1)
-        chain_m(0, 1)
-        chain_p(1)
-        zrow(0, 2)
-        zrow(0, 3)
+        for n in range(3):
+            zrow(0, n)
         new_sums(2)
-        for n in range(NB):
+        for n in ROT:
             mx_block(2, n)
+        chain_m(0, 0)
         chain_t(1)
         chain_s(1)
         chain_d(1)
-        chain_b(0)
-        ssq(2, 0)
-        ssq(2, 1)
+        dot(2, 3)
+        ssq(2, 3)
         leaky(0, 0, 2)
+        chain_m(0, 1)
         chain_v(1, 0)
+        ssq(2, 0)
         dot(2, 0)
         chain_v(1, 1)
-        dot(2, 1)
+        chain_b(0)
+        ssq(2, 1)
+        leaky(0, 2, 2)
         chain_v(1, 2)
         chain_g(1)
-        chain_n(1)
         ssq(2, 2)
-        leaky(0, 2, 2)
-        ssq(2, 3)
+        dot(2, 1)
+        chain_a(2)
+        shifted(1)
+        chain_n(1)
         dot(2, 2)
-        chain_m(1, 0)
-        dot(2, 3)
+        chain_t(2)
 
         for r in range(1, NT):
             last = r == NT - 1
-            if not last:
+            if r > 1 and not last:
                 chain_a(r + 1)
             if 1 < r and not last:
+                dot(r + 1, 3)
                 dot(r + 1, 0)
-            chain_m(r, 1)
-            chain_p(r + 1)
-            if 1 < r and not last:
-                dot(r + 1, 1)
+            chain_m(r, 0)
             scale_store(r - 1, 0, 2)
-            if not last:
+            if r > 1 and not last:
                 chain_t(r + 1)
-            chain_b(r)
             scale_store(r - 1, 2, 2)
             if not last:
                 chain_s(r + 1)
                 if 1 < r:
+                    dot(r + 1, 1)
                     dot(r + 1, 2)
-                    dot(r + 1, 3)
                 chain_d(r + 1)
-            for n in range(NB):
+            chain_m(r, 1)
+            for n in range(3):
                 zrow(r, n)
-                if not last and n < 3:
+                if not last:
                     chain_v(r + 1, n)
                 if last:
                     leaky(r, n, 1)
-                    scale_store(r, n, 1)
             if last:
+                chain_b(r)
+                leaky(r, 3, 1)
+                for n in range(NB):
+                    scale_store(r, n, 1)
                 break
             if r + 2 < NT:
                 new_sums(r + 2)
-                for n in range(NB):
+                for n in ROT:
                     mx_block(r + 2, n)
+                ssq(r + 2, 3)
                 ssq(r + 2, 0)
-                ssq(r + 2, 1)
+            chain_b(r)
             chain_g(r + 1)
+            if r + 2 < NT:
+                ssq(r + 2, 1)
+            shifted(r + 1)
             chain_n(r + 1)
             if r + 2 < NT:
                 ssq(r + 2, 2)
-                ssq(r + 2, 3)
             leaky(r, 0, 2)
             leaky(r, 2, 2)
-            chain_m(r + 1, 0)

@@ -20,13 +20,13 @@ NG = DIN // 512
 NT = B // P
 NB = DOUT // 512
 
-ORDER = [(s[0], int(s[1])) for s in "w0 x0 w1 w2 x1 w3 w4 x2 w5 w6 w7 x3".split()]
-W_PAT = ["FSFF"] * 8
-X_PAT = ["SSSS", "VSVS", "VSVS", "VVVV"]
+ORDER = [(s[0], int(s[1])) for s in "w0 x0 w1 w2 x1 w3 x2 w4 w5 w6 w7 x3".split()]
+W_PAT = ["FSFF"] * 5 + ["FSFS"] * 3
+X_PAT = ["SSSS", "SVSV", "SVSV", "VVVV"]
 T_BANKS = [4, 5, 6, 7, 3]
 EARLY = 3
-NORM_RATE = [0, 0, 2, 2, 2, 2, 2, 3, 3, 0, 0, 0]
-LOADS = [(s[0], int(s[1])) for s in "w0 x0 w1 x1 w2 x2 w3 x3 w4 w5 w6 w7".split()]
+NORM_RATE = [0, 2, 2, 2, 2, 2, 2, 2, 2, 0, 0, 0]
+LOADS = [(s[0], int(s[1])) for s in "w0 x0 w1 w2 x1 w3 x2 x3 w4 w5 w6 w7".split()]
 LAG = 1
 BIAS_AT = 4
 XN = (9, 10, 11)
@@ -345,6 +345,9 @@ def tile_hypequalizedlinear_kernel(tc, x, weight, bias, out):
             sl = slice(1536, 2048)
             nc.scalar.activation(out=zt[r][:, sl], in_=banks[(r, 3)][:], func=ACT.Copy,
                                  scale=coef[r]["ga"][:, 0:1])
+
+        def add_bias(r):
+            sl = slice(1536, 2048)
             ge.tensor_tensor(out=zt[r][:, sl], in0=zt[r][:, sl], in1=bias_l[:], op=ALU.add)
 
         def leaky(r, n, k):
@@ -441,6 +444,7 @@ def tile_hypequalizedlinear_kernel(tc, x, weight, bias, out):
         chain_v(0, 2)
         chain_g(0)
         shifted(0)
+        add_bias(0)
         ssq(1, 2)
         chain_n(0)
         dot(1, 3)
@@ -480,6 +484,7 @@ def tile_hypequalizedlinear_kernel(tc, x, weight, bias, out):
             last = r == NT - 1
             if r > 1 and not last:
                 chain_a(r + 1)
+            add_bias(r)
             if 1 < r and not last:
                 dot(r + 1, 3)
                 dot(r + 1, 0)

@@ -21,11 +21,11 @@ NT = B // P
 NB = DOUT // 512
 
 ORDER = [(s[0], int(s[1])) for s in "w0 x0 w1 w2 x1 w3 x2 w4 w5 w6 w7 x3".split()]
-W_PAT = ["FSFF"] * 5 + ["FSFS"] * 3
-X_PAT = ["SSSS", "SVSV", "SVSV", "VVVV"]
+W_PAT = ["FSFF"] * 6 + ["FSSS"] * 2
+X_PAT = ["SSSV", "SVSV", "SVSV", "VVVV"]
 T_BANKS = [4, 5, 6, 7, 3]
 EARLY = 3
-NORM_RATE = [0, 2, 2, 2, 2, 2, 2, 2, 2, 0, 0, 0]
+NORM_RATE = [0, 2, 2, 1, 2, 2, 2, 3, 2, 0, 0, 0]
 LOADS = [(s[0], int(s[1])) for s in "w0 x0 w1 w2 x1 w3 x2 x3 w4 w5 w6 w7".split()]
 LAG = 1
 BIAS_AT = 4
@@ -83,8 +83,9 @@ def tile_hypequalizedlinear_kernel(tc, x, weight, bias, out):
             t = pool.tile([P, 2, DIN], BF16, name="raw_" + kind, tag="raw_" + kind)
             raw[LOADS[i]] = t
             if i < 2:
-                for h in range(2):
-                    sl = slice(1024 * h, 1024 * h + 1024)
+                step = 512 if i == 0 else 1024
+                for h in range(DIN // step):
+                    sl = slice(step * h, step * h + step)
                     nc.sync.dma_start(out=t[:, :, sl], in_=view[c][:, :, sl])
             else:
                 nc.sync.dma_start(out=t[:], in_=view[c])
@@ -459,21 +460,21 @@ def tile_hypequalizedlinear_kernel(tc, x, weight, bias, out):
         chain_t(1)
         chain_s(1)
         chain_d(1)
+        leaky(0, 0, 2)
         dot(2, 3)
         ssq(2, 3)
-        leaky(0, 0, 2)
         chain_m(0, 1)
         chain_v(1, 0)
-        ssq(2, 0)
         dot(2, 0)
+        ssq(2, 0)
         chain_v(1, 1)
         chain_b(0)
         ssq(2, 1)
         leaky(0, 2, 2)
         chain_v(1, 2)
-        chain_g(1)
-        ssq(2, 2)
         dot(2, 1)
+        ssq(2, 2)
+        chain_g(1)
         chain_a(2)
         shifted(1)
         chain_n(1)
@@ -488,7 +489,6 @@ def tile_hypequalizedlinear_kernel(tc, x, weight, bias, out):
             if 1 < r and not last:
                 dot(r + 1, 3)
                 dot(r + 1, 0)
-            chain_m(r, 0)
             scale_store(r - 1, 0, 2)
             if r > 1 and not last:
                 chain_t(r + 1)
@@ -499,17 +499,17 @@ def tile_hypequalizedlinear_kernel(tc, x, weight, bias, out):
                     dot(r + 1, 1)
                     dot(r + 1, 2)
                 chain_d(r + 1)
-            chain_m(r, 1)
+            chain_m(r, 0)
             for n in range(3):
                 zrow(r, n)
+                if n == 0:
+                    chain_m(r, 1)
                 if not last:
                     chain_v(r + 1, n)
-                if last:
-                    leaky(r, n, 1)
             if last:
                 chain_b(r)
-                leaky(r, 3, 1)
                 for n in range(NB):
+                    leaky(r, n, 1)
                     scale_store(r, n, 1)
                 break
             if r + 2 < NT:

from contextlib import ExitStack

import concourse.bass as bass
import concourse.mybir as mybir
import concourse.tile as tile
from concourse.masks import make_identity

F32 = mybir.dt.float32
BF16 = mybir.dt.bfloat16
U32 = mybir.dt.uint32
U8 = mybir.dt.uint8
FP8X4 = mybir.dt.float8_e4m3fn_x4
ALU = mybir.AluOpType
ACT = mybir.ActivationFunctionType

P = 128
B, DIN, DOUT = 1024, 2048, 2048
FLOPS = 2 * B * DIN * DOUT
NG = DIN // 512
NT = B // P
NB = DOUT // 512

ORDER = [(s[0], int(s[1])) for s in "w0 x0 w1 w2 x1 w3 x2 w4 w5 w6 w7 x3".split()]
W_PAT = ["FSFF"] * 6 + ["FSSS"] * 2
X_PAT = ["SSSV", "SVSV", "SVSV", "VVVV"]
T_BANKS = [4, 5, 6, 7, 3]
EARLY = 3
NORM_RATE = [0, 2, 2, 1, 2, 2, 2, 3, 2, 0, 0, 0]
LOADS = [(s[0], int(s[1])) for s in "w0 x0 w1 w2 x1 w3 x2 x3 w4 w5 w6 w7".split()]
LAG = 1
BIAS_AT = 4
XN = (9, 10, 11)
NORM_ORDER = (0, 1, 2, 3)
AHEAD = 5


def tile_hypequalizedlinear_kernel(tc, x, weight, bias, out):
    nc = tc.nc
    x_v = x.rearrange("(c a p) k -> c p a k", a=2, p=P)
    w_v = weight.rearrange("(c a p) k -> c p a k", a=2, p=P)
    out_v = out.rearrange("(t p) n -> t p n", p=P)

    with ExitStack() as ctx:
        const = ctx.enter_context(tc.tile_pool(name="const", bufs=1))
        xin = ctx.enter_context(tc.tile_pool(name="xin", bufs=4))
        win = ctx.enter_context(tc.tile_pool(name="win", bufs=5))
        wsp = ctx.enter_context(tc.tile_pool(name="wsp", bufs=3))
        gp = ctx.enter_context(tc.tile_pool(name="gp", bufs=3))
        zp = ctx.enter_context(tc.tile_pool(name="zp", bufs=3))
        jkp = ctx.enter_context(tc.tile_pool(name="jkp", bufs=2))
        sm = ctx.enter_context(tc.tile_pool(name="sm", bufs=4))
        psum = ctx.enter_context(tc.psum_pool(name="psum", bufs=1))
        ctx.enter_context(tc.manual_schedule())

        ident = const.tile([P, P], F32, name="ident")
        make_identity(nc, ident[:])
        mh8 = const.tile([P, NT], F32, name="mh8")
        nc.gpsimd.memset(mh8[:], -0.5)
        tiny = const.tile([P, 1], F32, name="tiny")
        nc.gpsimd.memset(tiny[:], 2.0 ** -102)
        ones = const.tile([P, P], F32, name="ones")
        nc.gpsimd.memset(ones[:], 1.0)

        bias_l = const.tile([P, 512], F32, name="bias_l")
        bias_bc = const.tile([P, DOUT], BF16, name="bias_bc")
        bias_p = const.tile([P, DOUT // P], BF16, name="bias_p")
        xc = const.tile([P, 4, NG, 256], U32, name="xc", align_bytes=64)
        xs = const.tile([P, 4, NG, 256], U8, name="xs", align_bytes=64)
        wc = const.tile([P, NG, DOUT], U32, name="wc", align_bytes=64)
        ws = const.tile([P, NG, DOUT], U8, name="ws", align_bytes=64)
        xn2 = const.tile([P, 2, NT], F32, name="xn2")
        q = const.tile([P, NT], F32, name="q")
        y2 = const.tile([P, 1], F32, name="y2")
        nscb = const.tile([P, 1], F32, name="nscb")
        ny4 = const.tile([P, 1], F32, name="ny4")

        raw = {}

        def load(i):
            kind, c = LOADS[i]
            view = x_v if kind == "x" else w_v
            pool = xin if kind == "x" else win
            t = pool.tile([P, 2, DIN], BF16, name="raw_" + kind, tag="raw_" + kind)
            raw[LOADS[i]] = t
            if i < 2:
                step = 512 if i == 0 else 1024
                for h in range(DIN // step):
                    sl = slice(step * h, step * h + step)
                    nc.sync.dma_start(out=t[:, :, sl], in_=view[c][:, :, sl])
            else:
                nc.sync.dma_start(out=t[:], in_=view[c])

        grouped = {}

        turn = {"n": 0}

        scaled = {}

        def premult(i):
            if ORDER[i][0] == "x":
                return
            kind, c = ORDER[i]
            dry = [g for g in range(NG) if W_PAT[c][g] != "F"]
            if not dry:
                return
            sp = wsp.tile([P, 2, NG, 2, P, 2], BF16, name="sp", align_bytes=64)
            scaled[i] = sp
            src = raw[ORDER[i]][:].rearrange("q a (g p u e) -> q a g u p e", g=NG, u=2, e=2)
            if len(dry) == NG and i > 0:
                parts = [(sp[:].rearrange("q a g u p e -> q (a g) u p e")[:, :, u, :, :],
                          src.rearrange("q a g u p e -> q (a g) u p e")[:, :, u, :, :]) for u in range(2)]
            else:
                step = dry[1] - dry[0] if len(dry) > 1 else 1
                runs = [dry] if i > 0 and all(y - x == step for x, y in zip(dry, dry[1:])) else [[g] for g in dry]
                parts = [(sp[:, a, r[0]:r[-1] + 1:step, u, :, :], src[:, a, r[0]:r[-1] + 1:step, u, :, :])
                         for r in runs for u in range(2) for a in range(2)]
            for dst, s in parts:
                nc.vector.tensor_scalar(out=dst, in0=s, scalar1=0.1, scalar2=None, op0=ALU.mult)

        def transpose_and_copy(i):
            kind, c = ORDER[i]
            words = raw[ORDER[i]][:].bitcast(F32)
            if i in scaled:
                packed = scaled[i][:].rearrange("q a g u p e -> q a (g u p e)").bitcast(F32)
            gt = gp.tile([P, NG, 256, 4], BF16, name="gt", align_bytes=64)
            grouped[i] = gt
            for g in range(NG):
                tp = psum.tile([P, 2, 2, P], F32, tag="bk%d" % T_BANKS[turn["n"] % len(T_BANKS)], name="tp")
                turn["n"] += 1
                who = X_PAT[c][g] if kind == "x" else W_PAT[c][g]
                lo = 256 * g
                for u in range(2):
                    for a in range(2):
                        if kind == "w" and who != "F":
                            src = packed[:, a, lo + 128 * u:lo + 128 * u + 128]
                        else:
                            src = words[:, a, lo + u:lo + 256:2]
                        nc.tensor.transpose(tp[:, u, a, :], src, ident[:])
                wout = gt[:, g, :, :].bitcast(F32)
                win_ = tp[:].rearrange("p u a r -> p (a r) u")
                if who == "F":
                    nc.vector.tensor_scalar(
                        out=gt[:, g, :, :].rearrange("p j (u e) -> p j u e", e=2),
                        in0=tp[:].bitcast(BF16).rearrange("p u a (r e) -> p (a r) u e", e=2),
                        scalar1=0.1, scalar2=None, op0=ALU.mult)
                elif who == "V":
                    nc.vector.tensor_copy(out=wout, in_=win_)
                else:
                    nc.scalar.copy(out=wout, in_=win_)

        def quantise(i):
            kind, c = ORDER[i]
            gt = grouped[i]
            if kind == "x":
                nc.vector.quantize_mx(
                    out=xc[:, c, :, :].rearrange("p g j -> p (g j)").bitcast(FP8X4),
                    scales=xs[:, c, :, :].rearrange("p g j -> p (g j)"),
                    in_=gt[:].rearrange("p g j t -> p (g j t)"))
            else:
                for g in range(NG):
                    nc.vector.quantize_mx(
                        out=wc[:, g, 256 * c:256 * c + 256].bitcast(FP8X4),
                        scales=ws[:, g, 256 * c:256 * c + 256],
                        in_=gt[:, g, :, :].rearrange("p j t -> p (j t)"))

        def x_norm(c, a, h):
            jx = jkp.tile([P, 1024], BF16, name="jx", tag="jx")
            nc.scalar.activation(out=jx[:], in_=raw[("x", c)][:, a, 1024 * h:1024 * h + 1024], func=ACT.Square,
                                 accum_out=xn2[:, h, 2 * c + a:2 * c + a + 1])

        banks = {}

        def mx_block(r, n):
            acc = psum.tile([P, 512], F32, tag="bk%d" % (4 * (r % 2) + n), name="acc")
            banks[(r, n)] = acc
            c, a = r // 2, r % 2
            for g in range(NG):
                nc.tensor.matmul_mx(
                    out=acc[:],
                    lhsT=xc[:, c, g, 128 * a:128 * a + 128].bitcast(FP8X4),
                    lhsT_scale=xs[:, c, g, 128 * a:128 * a + 128],
                    rhs=wc[:, g, 512 * n:512 * n + 512].bitcast(FP8X4),
                    rhs_scale=ws[:, g, 512 * n:512 * n + 512],
                    start=(g == 0), stop=(g == NG - 1))

        ge = nc.gpsimd

        def col(nm, w=1):
            return sm.tile([P, w], F32, name=nm, tag=nm)

        xnt = {}

        def xn_batch1():
            xnt["xc2"], xnt["rxn"] = col("xc2", NT), col("rxn", NT)
            nc.vector.scalar_tensor_tensor(out=xnt["xc2"][:], in0=xn2[:, 0, :], scalar=1e-30, in1=xn2[:, 1, :],
                                           op0=ALU.max, op1=ALU.add)
            ge.tensor_tensor(out=xnt["rxn"][:], in0=xnt["xc2"][:], in1=mh8[:], op=ALU.pow)

        def xn_batch2():
            v, l1, l2, d = col("v8", NT), col("l1", NT), col("l2", NT), col("d8", NT)
            nc.vector.tensor_tensor(out=v[:], in0=xnt["xc2"][:], in1=xnt["rxn"][:], op=ALU.mult)
            nc.vector.tensor_scalar(out=v[:], in0=v[:], scalar1=1.0 - 1e-5, scalar2=None, op0=ALU.min)
            nc.scalar.activation(out=l1[:], in_=v[:], func=ACT.Ln, bias=1.0, scale=1.0)
            nc.scalar.activation(out=l2[:], in_=v[:], func=ACT.Ln, bias=1.0, scale=-1.0)
            xnt["d"], xnt["l"] = d, (l1, l2)

        def xn_batch3():
            (l1, l2), d = xnt["l"], xnt["d"]
            nc.vector.tensor_tensor(out=d[:], in0=l1[:], in1=l2[:], op=ALU.subtract)
            nc.vector.scalar_tensor_tensor(out=q[:], in0=d[:], scalar=0.5, in1=xnt["rxn"][:],
                                           op0=ALU.mult, op1=ALU.mult)

        def bias_map():
            jb = sm.tile([P, DOUT // P], F32, name="jb", bufs=1)
            sb = sm.tile([P, 1], F32, name="sb", bufs=1)
            nc.scalar.activation(out=jb[:], in_=bias_p[:], func=ACT.Square, accum_out=sb[:])
            tot = psum.tile([P, 1], F32, tag="bk0", name="tot")
            nc.tensor.matmul(out=tot[:], lhsT=ones[:], rhs=sb[:], start=True, stop=True)
            u2s = sm.tile([P, 1], F32, name="u2s", bufs=1)
            nc.scalar.activation(out=u2s[:], in_=tot[:], func=ACT.Copy, scale=0.01)
            u2 = sm.tile([P, 1], F32, name="u2", bufs=1)
            ge.tensor_scalar(out=u2[:], in0=u2s[:], scalar1=1e-30, scalar2=None, op0=ALU.max)
            run = sm.tile([P, 1], F32, name="run", bufs=1)
            ge.tensor_tensor(out=run[:], in0=u2[:], in1=mh8[:, 0:1], op=ALU.pow)
            return u2, run

        def bias_map2(u2, run):
            bmt["run"], bmt["tb"] = run, col("tb")
            nc.scalar.activation(out=bmt["tb"][:], in_=u2[:], func=ACT.Tanh, scale=run[:, 0:1])

        def bias_map3(i):
            tb = bmt["tb"]
            if i == 0:
                nc.vector.tensor_scalar(out=nscb[:], in0=tb[:], scalar1=bmt["run"][:, 0:1], scalar2=-0.1,
                                        op0=ALU.mult, op1=ALU.mult)
                nc.vector.tensor_tensor(out=y2[:], in0=tb[:], in1=tb[:], op=ALU.mult)
            elif i == 1:
                bmt["rnb"], bmt["y4"] = col("rnb"), col("y4")
                nc.vector.reciprocal(out=bmt["rnb"][:], in_=nscb[:])
                nc.vector.tensor_scalar(out=bmt["y4"][:], in0=y2[:], scalar1=1.0, scalar2=0.25,
                                        op0=ALU.add, op1=ALU.mult)
            else:
                nc.vector.tensor_tensor(out=ny4[:], in0=bmt["y4"][:], in1=bmt["rnb"][:], op=ALU.mult)

        bmt = {}
        sums = {}
        coef = {}
        zt = {}

        def new_sums(r):
            sums[r] = (sm.tile([P, NB], F32, name="ssq"), sm.tile([P, NB], F32, name="dot"))

        def ssq(r, n):
            js = jkp.tile([P, 512], F32, name="js", tag="js")
            nc.scalar.activation(out=js[:], in_=banks[(r, n)][:], func=ACT.Square,
                                 accum_out=sums[r][0][:, n:n + 1])

        def dot(r, n):
            jv = jkp.tile([P, 512], F32, name="jv", tag="jv")
            nc.vector.scalar_tensor_tensor(out=jv[:], in0=banks[(r, n)][:], scalar=-2.0,
                                           in1=bias_bc[:, 512 * n:512 * n + 512],
                                           op0=ALU.mult, op1=ALU.mult,
                                           accum_out=sums[r][1][:, n:n + 1])

        def chain_a(r):
            k = coef.setdefault(r, {})
            k["y"], k["yq"], k["rmn"] = col("y"), col("yq"), col("rmn")
            j4 = col("j4", NB)
            nc.scalar.activation(out=j4[:], in_=sums[r][0][:], func=ACT.Identity, bias=tiny[:, 0:1],
                                 accum_out=k["y"][:])
            nc.scalar.activation(out=k["yq"][:], in_=k["y"][:], func=ACT.Copy, scale=q[:, r:r + 1])
            ge.tensor_tensor(out=k["rmn"][:], in0=k["y"][:], in1=mh8[:, 0:1], op=ALU.pow)

        def chain_t(r):
            k = coef[r]
            k["th"], k["s"] = col("th"), col("s")
            nc.scalar.activation(out=k["th"][:], in_=k["yq"][:], func=ACT.Tanh, scale=k["rmn"][:, 0:1])

        def chain_s(r):
            k = coef[r]
            nc.scalar.activation(out=k["s"][:], in_=k["th"][:], func=ACT.Copy, scale=k["rmn"][:, 0:1])

        def chain_v(r, i):
            k = coef[r]
            if i == 0:
                k["a1"] = col("a1")
                nc.vector.tensor_scalar(out=k["a1"][:], in0=k["th"][:], scalar1=k["th"][:, 0:1], scalar2=1.0,
                                        op0=ALU.mult, op1=ALU.subtract)
            elif i == 1:
                k["nbc"] = col("nbc")
                nc.vector.tensor_scalar(out=k["nbc"][:], in0=k["a1"][:], scalar1=-1e-18, scalar2=None,
                                        op0=ALU.min)
            else:
                k["rn"] = col("rn")
                nc.vector.reciprocal(out=k["rn"][:], in_=k["nbc"][:])

        def chain_d(r):
            k = coef[r]
            k["t1"], k["ts"], k["xa"] = col("t1"), col("ts"), col("xa")
            j4 = col("j4", NB)
            nc.scalar.activation(out=j4[:], in_=sums[r][1][:], func=ACT.Identity, scale=k["s"][:, 0:1],
                                 bias=ny4[:, 0:1], accum_out=k["t1"][:])
            nc.scalar.activation(out=k["ts"][:], in_=k["t1"][:], func=ACT.Copy, scale=k["s"][:, 0:1])
            nc.scalar.activation(out=k["xa"][:], in_=k["t1"][:], func=ACT.Copy, scale=nscb[:, 0:1])

        def chain_g(r):
            k = coef[r]
            k["ga"] = col("ga")
            nc.scalar.activation(out=k["ga"][:], in_=k["ts"][:], func=ACT.Copy, scale=k["rn"][:, 0:1])

        def chain_n(r):
            k = coef[r]
            k["dn0"], k["dn1"], k["bcs"] = col("dn0"), col("dn1"), col("bcs")
            nc.scalar.activation(out=k["dn0"][:], in_=k["nbc"][:], func=ACT.Identity, scale=y2[:, 0:1],
                                 bias=k["xa"][:, 0:1])
            nc.scalar.activation(out=k["dn1"][:], in_=k["nbc"][:], func=ACT.Identity, bias=k["xa"][:, 0:1])
            nc.scalar.activation(out=k["bcs"][:], in_=k["nbc"][:], func=ACT.Copy, scale=nscb[:, 0:1])

        def chain_m(r, i):
            k = coef[r]
            if i == 0:
                k["mx"] = col("mx")
                nc.vector.tensor_scalar(out=k["mx"][:], in0=k["dn1"][:], scalar1=1.0 / (0.999 * 0.999),
                                        scalar2=k["dn0"][:, 0:1], op0=ALU.mult, op1=ALU.max)
            else:
                k["pd"], k["pr"] = col("pd"), col("pr")
                nc.vector.tensor_scalar(out=k["pd"][:], in0=k["mx"][:], scalar1=k["dn0"][:, 0:1],
                                        scalar2=1e-30, op0=ALU.mult, op1=ALU.max)
                ge.tensor_tensor(out=k["pr"][:], in0=k["pd"][:], in1=mh8[:, 0:1], op=ALU.pow)

        def chain_b(r):
            k = coef[r]
            k["be"] = col("be")
            nc.scalar.activation(out=k["be"][:], in_=k["pr"][:], func=ACT.Copy, scale=k["bcs"][:, 0:1])

        def zrow(r, n):
            if r not in zt:
                zt[r] = zp.tile([P, DOUT], F32, name="z", tag="z")
            sl = slice(512 * n, 512 * n + 512)
            nc.vector.scalar_tensor_tensor(out=zt[r][:, sl], in0=banks[(r, n)][:], scalar=coef[r]["ga"][:, 0:1],
                                           in1=bias_bc[:, sl], op0=ALU.mult, op1=ALU.add)

        def shifted(r):
            if r not in zt:
                zt[r] = zp.tile([P, DOUT], F32, name="z", tag="z")
            sl = slice(1536, 2048)
            nc.scalar.activation(out=zt[r][:, sl], in_=banks[(r, 3)][:], func=ACT.Copy,
                                 scale=coef[r]["ga"][:, 0:1])

        def add_bias(r):
            sl = slice(1536, 2048)
            ge.tensor_tensor(out=zt[r][:, sl], in0=zt[r][:, sl], in1=bias_l[:], op=ALU.add)

        def leaky(r, n, k):
            sl = slice(512 * n, 512 * (n + k))
            z = zt[r]
            nc.vector.scalar_tensor_tensor(out=z[:, sl], in0=z[:, sl], scalar=0.2,
                                           in1=z[:, sl], op0=ALU.mult, op1=ALU.max)

        def scale_store(r, n, k):
            sl = slice(512 * n, 512 * (n + k))
            z = zt[r]
            nc.scalar.activation(out=z[:, sl], in_=z[:, sl], func=ACT.Copy, scale=coef[r]["be"][:, 0:1])
            nc.sync.dma_start(out=out_v[r][:, sl], in_=z[:, sl])

        n_pairs = len(ORDER)
        norms = [(c, a, h) for c in NORM_ORDER for a in range(2) for h in range(2)]
        new_sums(0)
        pending_mm = []
        pending_dot = []
        for i in range(AHEAD):
            load(i)
            if i == 0:
                nc.sync.dma_start(out=bias_p[:], in_=bias.rearrange("(p j) -> p j", p=P))
            if i == BIAS_AT:
                nc.sync.dma_start(out=bias_bc[:], in_=bias.partition_broadcast(P))
        warm = sm.tile([P, 1], F32, name="warm", bufs=1)
        nc.scalar.activation(out=warm[:], in_=ones[:, 0:1], func=ACT.Ln)
        premult(0)
        for i in range(n_pairs):
            if i + AHEAD < n_pairs:
                load(i + AHEAD)
            for n in pending_dot:
                dot(0, n)
            if i >= LAG:
                quantise(i - LAG)
            transpose_and_copy(i)
            if i + 1 < n_pairs:
                premult(i + 1)
            if i == 6:
                nc.scalar.copy(out=bias_l[:], in_=bias_bc[:, 1536:2048])
            if i == 2:
                bm = bias_map()
            for n in pending_mm:
                mx_block(0, n)
            for n in pending_dot:
                ssq(0, n)
            pending_dot = pending_mm
            pending_mm = []
            if i >= LAG:
                kind, c = ORDER[i - LAG]
                if kind == "w" and c % 2 == 1 and c // 2 < EARLY:
                    pending_mm = [c // 2]
            for j in range(NORM_RATE[i]):
                if norms:
                    x_norm(*norms.pop(0))
            if i == XN[0]:
                xn_batch1()
            if i == XN[1]:
                xn_batch2()
            if i == XN[2]:
                bias_map2(*bm)
                xn_batch3()
        ROT = (3, 0, 1, 2)
        for n in pending_mm:
            mx_block(0, n)
        for n in pending_dot + pending_mm:
            dot(0, n)
            ssq(0, n)
        for i in range(n_pairs - LAG, n_pairs - 1):
            quantise(i)
        for n in range(EARLY, NB):
            mx_block(0, n)
            ssq(0, n)
        new_sums(1)
        bias_map3(0)
        for n in range(EARLY, NB):
            dot(0, n)
        bias_map3(1)
        chain_a(0)
        for n in range(NB):
            mx_block(1, n)
        dot(1, 0)
        bias_map3(2)
        dot(1, 1)
        chain_t(0)
        chain_s(0)
        ssq(1, 0)
        chain_v(0, 0)
        quantise(n_pairs - 1)
        chain_v(0, 1)
        chain_d(0)
        ssq(1, 1)
        dot(1, 2)
        chain_v(0, 2)
        chain_g(0)
        shifted(0)
        add_bias(0)
        ssq(1, 2)
        chain_n(0)
        dot(1, 3)
        ssq(1, 3)
        chain_a(1)
        for n in range(3):
            zrow(0, n)
        new_sums(2)
        for n in ROT:
            mx_block(2, n)
        chain_m(0, 0)
        chain_t(1)
        chain_s(1)
        chain_d(1)
        leaky(0, 0, 2)
        dot(2, 3)
        ssq(2, 3)
        chain_m(0, 1)
        chain_v(1, 0)
        dot(2, 0)
        ssq(2, 0)
        chain_v(1, 1)
        chain_b(0)
        ssq(2, 1)
        leaky(0, 2, 2)
        chain_v(1, 2)
        dot(2, 1)
        ssq(2, 2)
        chain_g(1)
        chain_a(2)
        shifted(1)
        chain_n(1)
        dot(2, 2)
        chain_t(2)

        for r in range(1, NT):
            last = r == NT - 1
            if r > 1 and not last:
                chain_a(r + 1)
            add_bias(r)
            if 1 < r and not last:
                dot(r + 1, 3)
                dot(r + 1, 0)
            scale_store(r - 1, 0, 2)
            if r > 1 and not last:
                chain_t(r + 1)
            scale_store(r - 1, 2, 2)
            if not last:
                chain_s(r + 1)
                if 1 < r:
                    dot(r + 1, 1)
                    dot(r + 1, 2)
                chain_d(r + 1)
            chain_m(r, 0)
            for n in range(3):
                zrow(r, n)
                if n == 0:
                    chain_m(r, 1)
                if not last:
                    chain_v(r + 1, n)
            if last:
                chain_b(r)
                for n in range(NB):
                    leaky(r, n, 1)
                    scale_store(r, n, 1)
                break
            if r + 2 < NT:
                new_sums(r + 2)
                for n in ROT:
                    mx_block(r + 2, n)
                ssq(r + 2, 3)
                ssq(r + 2, 0)
            chain_b(r)
            chain_g(r + 1)
            if r + 2 < NT:
                ssq(r + 2, 1)
            shifted(r + 1)
            chain_n(r + 1)
            if r + 2 < NT:
                ssq(r + 2, 2)
            leaky(r, 0, 2)
            leaky(r, 2, 2)
